import numpy as np
import ml_dtypes


def mxq(x, axis, fmt="e4m3"):
    dtype, down = {"e4m3": (ml_dtypes.float8_e4m3fn, 7), "e5m2": (ml_dtypes.float8_e5m2, 14)}[fmt]
    v = np.moveaxis(np.asarray(x, np.float32).astype(ml_dtypes.bfloat16).astype(np.float64), axis, -1)
    blocks = v.reshape(v.shape[:-1] + (-1, 32))
    amax = np.abs(blocks).max(-1, keepdims=True)
    byte = np.maximum(np.where(amax > 0, np.frexp(amax)[1] - 1 + 127, 0) - down, 1)
    scale = np.exp2(byte - 127.0)
    codes = (blocks / scale).astype(np.float32).astype(dtype).astype(np.float64)
    return np.moveaxis((codes * scale).reshape(v.shape), -1, axis)


WIDE = False


def mx_kscale(k):
    if not WIDE:
        return np.ones(k)
    levels = np.array([10, -10, 5, -5, 0])
    a = np.random.permutation(np.resize(levels, k // 512 * 4)).reshape(k // 512, 4)
    idx = np.arange(k)
    return np.exp2(a[idx // 512, idx % 128 // 32])


BF16 = ml_dtypes.bfloat16


def bf(x):
    return np.asarray(x, np.float32).astype(BF16)


def f64(x):
    return np.asarray(x).astype(np.float64)


N, D, K, R, ITERS = 4096, 512, 128, 3, 2
BETA = 5.0
NOISE = 0.7


def softmax_rows(v):
    e = np.exp(v - v.max(axis=1, keepdims=True))
    return e / e.sum(axis=1, keepdims=True)


def setup_inputs():
    s = mx_kscale(D)
    x = np.random.standard_normal((N, R)) @ np.random.standard_normal((R, D)) + NOISE * np.random.standard_normal((N, D))
    xn = x / np.sqrt((x * x).sum(axis=1, keepdims=True))
    return {"xn": bf(xn * s), "mu": bf(np.random.random((K, D)) / s)}


def reference(xn, mu):
    xn = f64(xn)
    logits = mxq(xn, 1, "e4m3") @ mxq(f64(mu), 1, "e4m3").T
    r = softmax_rows(BETA * logits)
    cluster_r = r.sum(axis=0)
    return (mxq(r, 0, "e4m3").T @ mxq(xn, 0, "e4m3")) / cluster_r[:, None]

@@ -1,0 +1,226 @@
+from contextlib import ExitStack
+
+import concourse.mybir as mybir
+from concourse.masks import make_identity
+
+F32 = mybir.dt.float32
+BF16 = mybir.dt.bfloat16
+U32 = mybir.dt.uint32
+U8 = mybir.dt.uint8
+FP8X4 = mybir.dt.float8_e4m3fn_x4
+AF = mybir.ActivationFunctionType
+ALU = mybir.AluOpType
+AX = mybir.AxisListType
+
+P = 128
+N_ROWS = 4096
+D = 512
+K = 128
+BETA = 5.0
+PACK = 4
+G = N_ROWS // (P * PACK)
+CS_N = 64
+S_COLS = [256,256,256,256,256,256,256,256]
+MANUAL = True
+
+FLOPS = 2 * 2 * N_ROWS * D * K
+
+
+def tile_clusternet_pa_kernel(tc, xn, mu, out):
+    nc = tc.nc
+    with ExitStack() as ctx:
+        keep = ctx.enter_context(tc.tile_pool(name="keep", bufs=1))
+        ps_t = ctx.enter_context(tc.psum_pool(name="ps_t", bufs=4))
+        ps_l = ctx.enter_context(tc.psum_pool(name="ps_l", bufs=2))
+        ps_o = ctx.enter_context(tc.psum_pool(name="ps_o", bufs=1))
+
+        x_sb = keep.tile([P, G, PACK, D], BF16, name="x_sb")
+        mu_sb = keep.tile([P, D], BF16, name="mu_sb")
+        ident = keep.tile([P, P], F32, name="ident")
+        xt_grp = keep.tile([P, G, PACK * P, PACK], BF16, name="xt_grp", align_bytes=64)
+        xt_codes = keep.tile([P, G, PACK * P], U32, name="xt_codes", align_bytes=64)
+        xt_scales = keep.tile([P, G, PACK * P], U8, name="xt_scales", align_bytes=64)
+        mu_grp = keep.tile([P, K, PACK], BF16, name="mu_grp", align_bytes=64)
+        mu_codes = keep.tile([P, K], U32, name="mu_codes", align_bytes=64)
+        mu_scales = keep.tile([P, K], U8, name="mu_scales", align_bytes=64)
+        xg = keep.tile([P, G, D, PACK], BF16, name="xg", align_bytes=64)
+        x2_codes = keep.tile([P, G, D], U32, name="x2_codes", align_bytes=64)
+        x2_scales = keep.tile([P, G, D], U8, name="x2_scales", align_bytes=64)
+        e_sb = keep.tile([P, G, PACK, K], F32, name="e_sb")
+        r_sb = keep.tile([P, G, K, PACK], BF16, name="r_sb", align_bytes=64)
+        r_codes = keep.tile([P, G, K], U32, name="r_codes", align_bytes=64)
+        r_scales = keep.tile([P, G, K], U8, name="r_scales", align_bytes=64)
+        mx = keep.tile([P, G, PACK], F32, name="mx")
+        nb = keep.tile([P, G, PACK], F32, name="nb")
+        sums = keep.tile([P, G, PACK], F32, name="sums")
+        rsum = keep.tile([P, G, PACK], F32, name="rsum")
+        warm_in = keep.tile([P, 1], F32, name="warm_in")
+        warm_out = keep.tile([P, 1], F32, name="warm_out")
+        rcs = keep.tile([P, 1], F32, name="rcs")
+        o_sb = keep.tile([P, D], F32, name="o_sb")
+
+        acc = ps_o.tile([P, D], F32, name="acc")
+        cs = ps_o.tile([P, CS_N], F32, name="cs")
+
+        banks = {}
+
+        def ok(g):
+            return 0 <= g < G
+
+        def load_x(g, j0, j1):
+            src = xn[g * P * PACK:(g + 1) * P * PACK, :].rearrange("(p j) d -> p j d", j=PACK)
+            nc.sync.dma_start(out=x_sb[:, g, j0:j1, :], in_=src[:, j0:j1, :])
+
+        def words_out(engine_copy, dst_bf16, bank, cols):
+            dst = dst_bf16.rearrange("p c t -> p (c t)").bitcast(F32).rearrange("p (c u) -> p c u", u=2)
+            engine_copy(out=dst, in_=bank[:, :, 0:cols].rearrange("p u c -> p c u"))
+
+        def t_mu():
+            tp = ps_t.tile([P, 2, 2 * P], F32, name="tp", tag="tp")
+            banks["mu"] = tp
+            for u in range(2):
+                nc.tensor.transpose(tp[:, u, 0:P], mu_sb[:].bitcast(F32)[:, u * P:(u + 1) * P], ident[:])
+
+        def c_mu():
+            words_out(nc.scalar.copy, mu_grp[:, :, :], banks["mu"], P)
+
+        def q_mu():
+            nc.vector.quantize_mx(out=mu_codes[:].bitcast(FP8X4), scales=mu_scales[:],
+                                  in_=mu_grp[:].rearrange("p c t -> p (c t)"))
+
+        def t_x(g):
+            if not ok(g):
+                return
+            for h in range(2):
+                tp = ps_t.tile([P, 2, 2 * P], F32, name="tp", tag="tp")
+                banks[(g, h)] = tp
+                for jj in range(2):
+                    xw = x_sb[:, g, 2 * h + jj, :].bitcast(F32)
+                    for u in range(2):
+                        nc.tensor.transpose(tp[:, u, jj * P:(jj + 1) * P], xw[:, u * P:(u + 1) * P], ident[:])
+
+        def c_x(g):
+            if not ok(g):
+                return
+            for h in range(2):
+                words_out(nc.scalar.copy, xt_grp[:, g, 2 * h * P:(2 * h + 2) * P, :], banks[(g, h)], 2 * P)
+
+        def q1(g):
+            if not ok(g):
+                return
+            nc.vector.quantize_mx(out=xt_codes[:, g, :].bitcast(FP8X4), scales=xt_scales[:, g, :],
+                                  in_=xt_grp[:, g, :, :].rearrange("p c t -> p (c t)"))
+
+        def m1(g):
+            if not ok(g):
+                return
+            lg = ps_l.tile([P, PACK, K], F32, name="lg", tag="lg")
+            banks[("l", g)] = lg
+            for j in range(PACK):
+                nc.tensor.matmul_mx(out=lg[:, j, :],
+                                    lhsT=xt_codes[:, g, j * P:(j + 1) * P].bitcast(FP8X4),
+                                    lhsT_scale=xt_scales[:, g, j * P:(j + 1) * P],
+                                    rhs=mu_codes[:].bitcast(FP8X4), rhs_scale=mu_scales[:],
+                                    start=True, stop=True)
+
+        def row_max(g):
+            if not ok(g):
+                return
+            nc.vector.tensor_reduce(out=mx[:, g, :], in_=banks[("l", g)][:], axis=AX.X, op=ALU.max)
+            nc.vector.tensor_scalar_mul(out=nb[:, g, :], in0=mx[:, g, :], scalar1=-BETA)
+
+        def expo(g):
+            if not ok(g):
+                return
+            lg = banks[("l", g)]
+            for j in range(PACK):
+                nc.scalar.activation(out=e_sb[:, g, j, :], in_=lg[:, j, :], func=AF.Exp,
+                                     bias=nb[:, g, j:j + 1], scale=BETA, accum_out=sums[:, g, j:j + 1])
+
+        def rcp(g):
+            if not ok(g):
+                return
+            nc.vector.reciprocal(rsum[:, g, :], sums[:, g, :])
+
+        def nrm(g):
+            if not ok(g):
+                return
+            nc.vector.tensor_tensor(out=r_sb[:, g, :, :], in0=e_sb[:, g, :, :].rearrange("p j k -> p k j"),
+                                    in1=rsum[:, g, :].unsqueeze(1).to_broadcast([P, K, PACK]), op=ALU.mult)
+
+        def colsum(g):
+            if not ok(g):
+                return
+            for j in range(PACK):
+                nc.tensor.matmul(out=cs[:], lhsT=e_sb[:, g, j, :],
+                                 rhs=rsum[:, g, j:j + 1].to_broadcast([P, CS_N]),
+                                 start=(g == 0 and j == 0), stop=(g == G - 1 and j == PACK - 1))
+
+        def q3(g):
+            if not ok(g):
+                return
+            nc.vector.quantize_mx(out=r_codes[:, g, :].bitcast(FP8X4), scales=r_scales[:, g, :],
+                                  in_=r_sb[:, g, :, :].rearrange("p k j -> p (k j)"))
+
+        def regroup(engine_copy, g, d0, d1):
+            if not ok(g) or d1 <= d0:
+                return
+            engine_copy(out=xg[:, g, d0:d1, :].rearrange("p (c i) t -> p c t i", i=4),
+                        in_=x_sb[:, g, :, d0:d1].rearrange("p t (c i) -> p c t i", i=4))
+
+        def rg_s(g):
+            if ok(g):
+                regroup(nc.scalar.copy, g, 0, S_COLS[g])
+
+        def rg_v(g):
+            if ok(g):
+                regroup(nc.vector.tensor_copy, g, S_COLS[g], D)
+
+        def q2(g):
+            if not ok(g):
+                return
+            nc.vector.quantize_mx(out=x2_codes[:, g, :].bitcast(FP8X4), scales=x2_scales[:, g, :],
+                                  in_=xg[:, g, :, :].rearrange("p d j -> p (d j)"))
+
+        def m2(g):
+            if not ok(g):
+                return
+            nc.tensor.matmul_mx(out=acc[:], lhsT=r_codes[:, g, :].bitcast(FP8X4), lhsT_scale=r_scales[:, g, :],
+                                rhs=x2_codes[:, g, :].bitcast(FP8X4), rhs_scale=x2_scales[:, g, :],
+                                start=(g == 0), stop=(g == G - 1))
+
+        if MANUAL:
+            ctx.enter_context(tc.manual_schedule())
+
+        nc.scalar.dma_start(out=mu_sb[:], in_=mu[:, :])
+        load_x(0, 0, 2)
+        load_x(0, 2, 4)
+        for g in range(1, G):
+            load_x(g, 0, PACK)
+        make_identity(nc, ident[:])
+        nc.vector.memset(warm_in[:], 0.0)
+        nc.scalar.activation(out=warm_out[:], in_=warm_in[:], func=AF.Exp)
+
+        t_mu()
+        c_mu()
+        q_mu()
+        t_x(0)
+        for t in range(G + 2):
+            t_x(t + 1)
+            c_x(t)
+            row_max(t - 1)
+            expo(t - 1)
+            rcp(t - 2)
+            nrm(t - 2)
+            colsum(t - 2)
+            q1(t)
+            m1(t)
+            q3(t - 2)
+            rg_v(t)
+            rg_s(t)
+            q2(t - 1)
+            m2(t - 2)
+
+        nc.vector.reciprocal(rcs[:], cs[:, 0:1])
+        nc.vector.tensor_scalar_mul(out=o_sb[:], in0=acc[:], scalar1=rcs[:, 0:1])
+        nc.sync.dma_start(out=out[:, :], in_=o_sb[:])

@@ -21,7 +21,7 @@ PACK = 4
 G = N_ROWS // (P * PACK)
 CS_N = 64
 S_COLS = [256,256,256,256,256,256,256,256]
-MANUAL = True
+MANUAL = False
 
 FLOPS = 2 * 2 * N_ROWS * D * K
 

@@ -19,7 +19,6 @@ K = 128
 BETA = 5.0
 PACK = 4
 G = N_ROWS // (P * PACK)
-CS_N = 64
 S_COLS = [256,256,256,256,256,256,256,256]
 MANUAL = False
 
@@ -47,6 +46,7 @@ def tile_clusternet_pa_kernel(tc, xn, mu, out):
         x2_codes = keep.tile([P, G, D], U32, name="x2_codes", align_bytes=64)
         x2_scales = keep.tile([P, G, D], U8, name="x2_scales", align_bytes=64)
         e_sb = keep.tile([P, G, PACK, K], F32, name="e_sb")
+        r32 = keep.tile([P, G, PACK, K], F32, name="r32")
         r_sb = keep.tile([P, G, K, PACK], BF16, name="r_sb", align_bytes=64)
         r_codes = keep.tile([P, G, K], U32, name="r_codes", align_bytes=64)
         r_scales = keep.tile([P, G, K], U8, name="r_scales", align_bytes=64)
@@ -60,7 +60,8 @@ def tile_clusternet_pa_kernel(tc, xn, mu, out):
         o_sb = keep.tile([P, D], F32, name="o_sb")
 
         acc = ps_o.tile([P, D], F32, name="acc")
-        cs = ps_o.tile([P, CS_N], F32, name="cs")
+        st = ps_o.tile([P, P], F32, name="st")
+        cs_sb = keep.tile([P, 1], F32, name="cs_sb")
 
         banks = {}
 
@@ -145,15 +146,19 @@ def tile_clusternet_pa_kernel(tc, xn, mu, out):
         def nrm(g):
             if not ok(g):
                 return
-            nc.vector.tensor_tensor(out=r_sb[:, g, :, :], in0=e_sb[:, g, :, :].rearrange("p j k -> p k j"),
-                                    in1=rsum[:, g, :].unsqueeze(1).to_broadcast([P, K, PACK]), op=ALU.mult)
+            for j in range(PACK):
+                nc.vector.tensor_scalar_mul(out=r32[:, g, j, :], in0=e_sb[:, g, j, :], scalar1=rsum[:, g, j:j + 1])
+
+        def cast(g):
+            if not ok(g):
+                return
+            nc.vector.tensor_copy(out=r_sb[:, g, :, :], in_=r32[:, g, :, :].rearrange("p j k -> p k j"))
 
         def colsum(g):
             if not ok(g):
                 return
             for j in range(PACK):
-                nc.tensor.matmul(out=cs[:], lhsT=e_sb[:, g, j, :],
-                                 rhs=rsum[:, g, j:j + 1].to_broadcast([P, CS_N]),
+                nc.tensor.matmul(out=st[:], lhsT=r32[:, g, j, :], rhs=ident[:], is_transpose=True,
                                  start=(g == 0 and j == 0), stop=(g == G - 1 and j == PACK - 1))
 
         def q3(g):
@@ -215,12 +220,14 @@ def tile_clusternet_pa_kernel(tc, xn, mu, out):
             colsum(t - 2)
             q1(t)
             m1(t)
-            q3(t - 2)
+            cast(t - 2)
             rg_v(t)
             rg_s(t)
+            q3(t - 2)
             q2(t - 1)
             m2(t - 2)
 
-        nc.vector.reciprocal(rcs[:], cs[:, 0:1])
+        nc.vector.tensor_reduce(out=cs_sb[:], in_=st[:], axis=AX.X, op=ALU.add)
+        nc.vector.reciprocal(rcs[:], cs_sb[:])
         nc.vector.tensor_scalar_mul(out=o_sb[:], in0=acc[:], scalar1=rcs[:, 0:1])
         nc.sync.dma_start(out=out[:, :], in_=o_sb[:])

@@ -19,8 +19,7 @@ K = 128
 BETA = 5.0
 PACK = 4
 G = N_ROWS // (P * PACK)
-S_COLS = [256,256,256,256,256,256,256,256]
-MANUAL = False
+MANUAL = True
 
 FLOPS = 2 * 2 * N_ROWS * D * K
 
@@ -29,8 +28,7 @@ def tile_clusternet_pa_kernel(tc, xn, mu, out):
     nc = tc.nc
     with ExitStack() as ctx:
         keep = ctx.enter_context(tc.tile_pool(name="keep", bufs=1))
-        ps_t = ctx.enter_context(tc.psum_pool(name="ps_t", bufs=4))
-        ps_l = ctx.enter_context(tc.psum_pool(name="ps_l", bufs=2))
+        ps_b = ctx.enter_context(tc.psum_pool(name="ps_b", bufs=6))
         ps_o = ctx.enter_context(tc.psum_pool(name="ps_o", bufs=1))
 
         x_sb = keep.tile([P, G, PACK, D], BF16, name="x_sb")
@@ -77,7 +75,7 @@ def tile_clusternet_pa_kernel(tc, xn, mu, out):
             engine_copy(out=dst, in_=bank[:, :, 0:cols].rearrange("p u c -> p c u"))
 
         def t_mu():
-            tp = ps_t.tile([P, 2, 2 * P], F32, name="tp", tag="tp")
+            tp = ps_b.tile([P, 2, 2 * P], F32, name="tp", tag="bank")
             banks["mu"] = tp
             for u in range(2):
                 nc.tensor.transpose(tp[:, u, 0:P], mu_sb[:].bitcast(F32)[:, u * P:(u + 1) * P], ident[:])
@@ -89,22 +87,16 @@ def tile_clusternet_pa_kernel(tc, xn, mu, out):
             nc.vector.quantize_mx(out=mu_codes[:].bitcast(FP8X4), scales=mu_scales[:],
                                   in_=mu_grp[:].rearrange("p c t -> p (c t)"))
 
-        def t_x(g):
-            if not ok(g):
-                return
-            for h in range(2):
-                tp = ps_t.tile([P, 2, 2 * P], F32, name="tp", tag="tp")
-                banks[(g, h)] = tp
-                for jj in range(2):
-                    xw = x_sb[:, g, 2 * h + jj, :].bitcast(F32)
-                    for u in range(2):
-                        nc.tensor.transpose(tp[:, u, jj * P:(jj + 1) * P], xw[:, u * P:(u + 1) * P], ident[:])
+        def t_x(g, h):
+            tp = ps_b.tile([P, 2, 2 * P], F32, name="tp", tag="bank")
+            banks[(g, h)] = tp
+            for jj in range(2):
+                xw = x_sb[:, g, 2 * h + jj, :].bitcast(F32)
+                for u in range(2):
+                    nc.tensor.transpose(tp[:, u, jj * P:(jj + 1) * P], xw[:, u * P:(u + 1) * P], ident[:])
 
-        def c_x(g):
-            if not ok(g):
-                return
-            for h in range(2):
-                words_out(nc.scalar.copy, xt_grp[:, g, 2 * h * P:(2 * h + 2) * P, :], banks[(g, h)], 2 * P)
+        def c_x(g, h):
+            words_out(nc.scalar.copy, xt_grp[:, g, 2 * h * P:(2 * h + 2) * P, :], banks[(g, h)], 2 * P)
 
         def q1(g):
             if not ok(g):
@@ -115,7 +107,7 @@ def tile_clusternet_pa_kernel(tc, xn, mu, out):
         def m1(g):
             if not ok(g):
                 return
-            lg = ps_l.tile([P, PACK, K], F32, name="lg", tag="lg")
+            lg = ps_b.tile([P, PACK, K], F32, name="lg", tag="bank")
             banks[("l", g)] = lg
             for j in range(PACK):
                 nc.tensor.matmul_mx(out=lg[:, j, :],
@@ -144,22 +136,20 @@ def tile_clusternet_pa_kernel(tc, xn, mu, out):
             nc.vector.reciprocal(rsum[:, g, :], sums[:, g, :])
 
         def nrm(g):
-            if not ok(g):
-                return
             for j in range(PACK):
                 nc.vector.tensor_scalar_mul(out=r32[:, g, j, :], in0=e_sb[:, g, j, :], scalar1=rsum[:, g, j:j + 1])
 
         def cast(g):
-            if not ok(g):
-                return
             nc.vector.tensor_copy(out=r_sb[:, g, :, :], in_=r32[:, g, :, :].rearrange("p j k -> p k j"))
 
         def colsum(g):
-            if not ok(g):
-                return
             for j in range(PACK):
                 nc.tensor.matmul(out=st[:], lhsT=r32[:, g, j, :], rhs=ident[:], is_transpose=True,
                                  start=(g == 0 and j == 0), stop=(g == G - 1 and j == PACK - 1))
+
+        def col_recip():
+            nc.vector.tensor_reduce(out=cs_sb[:], in_=st[:], axis=AX.X, op=ALU.add)
+            nc.vector.reciprocal(rcs[:], cs_sb[:])
 
         def q3(g):
             if not ok(g):
@@ -173,13 +163,11 @@ def tile_clusternet_pa_kernel(tc, xn, mu, out):
             engine_copy(out=xg[:, g, d0:d1, :].rearrange("p (c i) t -> p c t i", i=4),
                         in_=x_sb[:, g, :, d0:d1].rearrange("p t (c i) -> p c t i", i=4))
 
-        def rg_s(g):
-            if ok(g):
-                regroup(nc.scalar.copy, g, 0, S_COLS[g])
+        def rg_s(g, d0, d1):
+            regroup(nc.scalar.copy, g, d0, d1)
 
-        def rg_v(g):
-            if ok(g):
-                regroup(nc.vector.tensor_copy, g, S_COLS[g], D)
+        def rg_v(g, d0, d1):
+            regroup(nc.vector.tensor_copy, g, d0, d1)
 
         def q2(g):
             if not ok(g):
@@ -207,27 +195,147 @@ def tile_clusternet_pa_kernel(tc, xn, mu, out):
         nc.scalar.activation(out=warm_out[:], in_=warm_in[:], func=AF.Exp)
 
         t_mu()
+        t_x(0, 0)
         c_mu()
+        rg_v(0, 128, 256)
         q_mu()
-        t_x(0)
-        for t in range(G + 2):
-            t_x(t + 1)
-            c_x(t)
-            row_max(t - 1)
-            expo(t - 1)
-            rcp(t - 2)
-            nrm(t - 2)
-            colsum(t - 2)
-            q1(t)
-            m1(t)
-            cast(t - 2)
-            rg_v(t)
-            rg_s(t)
-            q3(t - 2)
-            q2(t - 1)
-            m2(t - 2)
+        rg_s(0, 0, 128)
+        t_x(0, 1)
+        rg_v(0, 256, 512)
+        c_x(0, 0)
+        rg_v(1, 128, 256)
+        t_x(1, 0)
+        c_x(0, 1)
+        q2(0)
+        rg_v(1, 256, 384)
+        t_x(1, 1)
+        rg_s(1, 0, 128)
+        q1(0)
+        c_x(1, 0)
+        t_x(2, 0)
+        rg_v(1, 384, 512)
+        rg_v(2, 0, 128)
+        c_x(1, 1)
+        t_x(2, 1)
+        q2(1)
+        c_x(2, 0)
+        t_x(3, 0)
+        q1(1)
+        c_x(2, 1)
+        rg_v(2, 128, 384)
+        t_x(3, 1)
+        c_x(3, 0)
+        t_x(4, 0)
+        q1(2)
+        c_x(3, 1)
+        rg_v(2, 384, 512)
+        t_x(4, 1)
+        c_x(4, 0)
+        q1(3)
+        t_x(5, 0)
+        c_x(4, 1)
+        q2(2)
+        t_x(5, 1)
+        c_x(5, 0)
+        q1(4)
+        t_x(6, 0)
+        rg_v(3, 0, 256)
+        c_x(5, 1)
+        t_x(6, 1)
+        c_x(6, 0)
+        q1(5)
+        t_x(7, 0)
+        rg_v(3, 256, 512)
+        c_x(6, 1)
+        t_x(7, 1)
+        c_x(7, 0)
+        q1(6)
+        m1(0)
+        c_x(7, 1)
+        q2(3)
+        m1(1)
+        rg_s(4, 0, 384)
+        q1(7)
+        m1(2)
+        row_max(0)
+        m1(3)
+        row_max(1)
+        m1(4)
+        expo(0)
+        row_max(2)
+        m1(5)
+        row_max(3)
+        m1(6)
+        expo(1)
+        row_max(4)
+        m1(7)
+        expo(2)
+        row_max(5)
+        row_max(6)
+        expo(3)
+        row_max(7)
+        rcp(0)
+        nrm(0)
+        expo(4)
+        rcp(1)
+        nrm(1)
+        rcp(2)
+        nrm(2)
+        expo(5)
+        rcp(3)
+        colsum(0)
+        nrm(3)
+        rcp(4)
+        colsum(1)
+        nrm(4)
+        expo(6)
+        rcp(5)
+        nrm(5)
+        rcp(6)
+        colsum(2)
+        nrm(6)
+        expo(7)
+        colsum(3)
+        cast(0)
+        rcp(7)
+        rg_s(4, 384, 512)
+        nrm(7)
+        colsum(4)
+        cast(1)
+        rg_s(5, 0, 512)
+        q3(0)
+        cast(2)
+        colsum(5)
+        q3(1)
+        cast(3)
+        q3(2)
+        colsum(6)
+        cast(4)
+        q3(3)
+        colsum(7)
+        cast(5)
+        q3(4)
+        rg_s(6, 0, 512)
+        col_recip()
+        m2(0)
+        cast(6)
+        q3(5)
+        m2(1)
+        cast(7)
+        q3(6)
+        m2(2)
+        q2(4)
+        q3(7)
+        m2(3)
+        rg_v(7, 384, 512)
+        rg_s(7, 0, 384)
+        m2(4)
+        q2(5)
+        q2(6)
+        m2(5)
+        m2(6)
+        q2(7)
+        m2(7)
 
-        nc.vector.tensor_reduce(out=cs_sb[:], in_=st[:], axis=AX.X, op=ALU.add)
-        nc.vector.reciprocal(rcs[:], cs_sb[:])
         nc.vector.tensor_scalar_mul(out=o_sb[:], in0=acc[:], scalar1=rcs[:, 0:1])
         nc.sync.dma_start(out=out[:, :], in_=o_sb[:])

@@ -19,7 +19,6 @@ K = 128
 BETA = 5.0
 PACK = 4
 G = N_ROWS // (P * PACK)
-MANUAL = True
 
 FLOPS = 2 * 2 * N_ROWS * D * K
 
@@ -54,25 +53,23 @@ def tile_clusternet_pa_kernel(tc, xn, mu, out):
         rsum = keep.tile([P, G, PACK], F32, name="rsum")
         warm_in = keep.tile([P, 1], F32, name="warm_in")
         warm_out = keep.tile([P, 1], F32, name="warm_out")
+        anchor = keep.tile([P, 2], F32, name="anchor")
+        cs_sb = keep.tile([P, 1], F32, name="cs_sb")
         rcs = keep.tile([P, 1], F32, name="rcs")
         o_sb = keep.tile([P, D], F32, name="o_sb")
 
         acc = ps_o.tile([P, D], F32, name="acc")
         st = ps_o.tile([P, P], F32, name="st")
-        cs_sb = keep.tile([P, 1], F32, name="cs_sb")
 
         banks = {}
-
-        def ok(g):
-            return 0 <= g < G
 
         def load_x(g, j0, j1):
             src = xn[g * P * PACK:(g + 1) * P * PACK, :].rearrange("(p j) d -> p j d", j=PACK)
             nc.sync.dma_start(out=x_sb[:, g, j0:j1, :], in_=src[:, j0:j1, :])
 
-        def words_out(engine_copy, dst_bf16, bank, cols):
+        def words_out(dst_bf16, bank, cols):
             dst = dst_bf16.rearrange("p c t -> p (c t)").bitcast(F32).rearrange("p (c u) -> p c u", u=2)
-            engine_copy(out=dst, in_=bank[:, :, 0:cols].rearrange("p u c -> p c u"))
+            nc.scalar.copy(out=dst, in_=bank[:, :, 0:cols].rearrange("p u c -> p c u"))
 
         def t_mu():
             tp = ps_b.tile([P, 2, 2 * P], F32, name="tp", tag="bank")
@@ -81,7 +78,7 @@ def tile_clusternet_pa_kernel(tc, xn, mu, out):
                 nc.tensor.transpose(tp[:, u, 0:P], mu_sb[:].bitcast(F32)[:, u * P:(u + 1) * P], ident[:])
 
         def c_mu():
-            words_out(nc.scalar.copy, mu_grp[:, :, :], banks["mu"], P)
+            words_out(mu_grp[:, :, :], banks["mu"], P)
 
         def q_mu():
             nc.vector.quantize_mx(out=mu_codes[:].bitcast(FP8X4), scales=mu_scales[:],
@@ -96,17 +93,13 @@ def tile_clusternet_pa_kernel(tc, xn, mu, out):
                     nc.tensor.transpose(tp[:, u, jj * P:(jj + 1) * P], xw[:, u * P:(u + 1) * P], ident[:])
 
         def c_x(g, h):
-            words_out(nc.scalar.copy, xt_grp[:, g, 2 * h * P:(2 * h + 2) * P, :], banks[(g, h)], 2 * P)
+            words_out(xt_grp[:, g, 2 * h * P:(2 * h + 2) * P, :], banks[(g, h)], 2 * P)
 
         def q1(g):
-            if not ok(g):
-                return
             nc.vector.quantize_mx(out=xt_codes[:, g, :].bitcast(FP8X4), scales=xt_scales[:, g, :],
                                   in_=xt_grp[:, g, :, :].rearrange("p c t -> p (c t)"))
 
         def m1(g):
-            if not ok(g):
-                return
             lg = ps_b.tile([P, PACK, K], F32, name="lg", tag="bank")
             banks[("l", g)] = lg
             for j in range(PACK):
@@ -116,23 +109,21 @@ def tile_clusternet_pa_kernel(tc, xn, mu, out):
                                     rhs=mu_codes[:].bitcast(FP8X4), rhs_scale=mu_scales[:],
                                     start=True, stop=True)
 
+        def window():
+            nc.vector.memset(anchor[:, 0:1], 1.0)
+            nc.vector.memset(anchor[:, 1:2], 0.0)
+
         def row_max(g):
-            if not ok(g):
-                return
             nc.vector.tensor_reduce(out=mx[:, g, :], in_=banks[("l", g)][:], axis=AX.X, op=ALU.max)
-            nc.vector.tensor_scalar_mul(out=nb[:, g, :], in0=mx[:, g, :], scalar1=-BETA)
 
         def expo(g):
-            if not ok(g):
-                return
             lg = banks[("l", g)]
+            nc.scalar.mul(nb[:, g, :], mx[:, g, :], -BETA)
             for j in range(PACK):
                 nc.scalar.activation(out=e_sb[:, g, j, :], in_=lg[:, j, :], func=AF.Exp,
                                      bias=nb[:, g, j:j + 1], scale=BETA, accum_out=sums[:, g, j:j + 1])
 
         def rcp(g):
-            if not ok(g):
-                return
             nc.vector.reciprocal(rsum[:, g, :], sums[:, g, :])
 
         def nrm(g):
@@ -141,6 +132,9 @@ def tile_clusternet_pa_kernel(tc, xn, mu, out):
 
         def cast(g):
             nc.vector.tensor_copy(out=r_sb[:, g, :, :], in_=r32[:, g, :, :].rearrange("p j k -> p k j"))
+
+        def cast_s(g):
+            nc.scalar.copy(out=r_sb[:, g, :, :], in_=r32[:, g, :, :].rearrange("p j k -> p k j"))
 
         def colsum(g):
             for j in range(PACK):
@@ -152,14 +146,10 @@ def tile_clusternet_pa_kernel(tc, xn, mu, out):
             nc.vector.reciprocal(rcs[:], cs_sb[:])
 
         def q3(g):
-            if not ok(g):
-                return
             nc.vector.quantize_mx(out=r_codes[:, g, :].bitcast(FP8X4), scales=r_scales[:, g, :],
                                   in_=r_sb[:, g, :, :].rearrange("p k j -> p (k j)"))
 
         def regroup(engine_copy, g, d0, d1):
-            if not ok(g) or d1 <= d0:
-                return
             engine_copy(out=xg[:, g, d0:d1, :].rearrange("p (c i) t -> p c t i", i=4),
                         in_=x_sb[:, g, :, d0:d1].rearrange("p t (c i) -> p c t i", i=4))
 
@@ -169,21 +159,20 @@ def tile_clusternet_pa_kernel(tc, xn, mu, out):
         def rg_v(g, d0, d1):
             regroup(nc.vector.tensor_copy, g, d0, d1)
 
+        def rg_g(g, d0, d1):
+            nc.gpsimd.tensor_scalar(out=xg[:, g, d0:d1, :], in0=x_sb[:, g, :, d0:d1].rearrange("p t d -> p d t"),
+                                    scalar1=anchor[:, 0:1], scalar2=anchor[:, 1:2], op0=ALU.mult, op1=ALU.add)
+
         def q2(g):
-            if not ok(g):
-                return
             nc.vector.quantize_mx(out=x2_codes[:, g, :].bitcast(FP8X4), scales=x2_scales[:, g, :],
                                   in_=xg[:, g, :, :].rearrange("p d j -> p (d j)"))
 
         def m2(g):
-            if not ok(g):
-                return
             nc.tensor.matmul_mx(out=acc[:], lhsT=r_codes[:, g, :].bitcast(FP8X4), lhsT_scale=r_scales[:, g, :],
                                 rhs=x2_codes[:, g, :].bitcast(FP8X4), rhs_scale=x2_scales[:, g, :],
                                 start=(g == 0), stop=(g == G - 1))
 
-        if MANUAL:
-            ctx.enter_context(tc.manual_schedule())
+        ctx.enter_context(tc.manual_schedule())
 
         nc.scalar.dma_start(out=mu_sb[:], in_=mu[:, :])
         load_x(0, 0, 2)
@@ -197,11 +186,11 @@ def tile_clusternet_pa_kernel(tc, xn, mu, out):
         t_mu()
         t_x(0, 0)
         c_mu()
-        rg_v(0, 128, 256)
+        rg_v(0, 128, 384)
+        t_x(0, 1)
         q_mu()
         rg_s(0, 0, 128)
-        t_x(0, 1)
-        rg_v(0, 256, 512)
+        rg_v(0, 384, 512)
         c_x(0, 0)
         rg_v(1, 128, 256)
         t_x(1, 0)
@@ -214,127 +203,130 @@ def tile_clusternet_pa_kernel(tc, xn, mu, out):
         c_x(1, 0)
         t_x(2, 0)
         rg_v(1, 384, 512)
-        rg_v(2, 0, 128)
+        rg_v(2, 128, 256)
         c_x(1, 1)
         t_x(2, 1)
         q2(1)
         c_x(2, 0)
         t_x(3, 0)
         q1(1)
-        c_x(2, 1)
-        rg_v(2, 128, 384)
+        rg_s(2, 0, 128)
+        rg_v(2, 256, 512)
         t_x(3, 1)
-        c_x(3, 0)
+        c_x(2, 1)
+        rg_v(3, 0, 128)
         t_x(4, 0)
-        q1(2)
-        c_x(3, 1)
-        rg_v(2, 384, 512)
-        t_x(4, 1)
-        c_x(4, 0)
-        q1(3)
-        t_x(5, 0)
-        c_x(4, 1)
+        c_x(3, 0)
         q2(2)
+        t_x(4, 1)
+        c_x(3, 1)
+        q1(2)
+        c_x(4, 0)
+        t_x(5, 0)
+        rg_v(3, 128, 256)
+        c_x(4, 1)
+        q1(3)
         t_x(5, 1)
+        rg_v(3, 256, 512)
         c_x(5, 0)
-        q1(4)
         t_x(6, 0)
-        rg_v(3, 0, 256)
         c_x(5, 1)
+        q1(4)
         t_x(6, 1)
+        rg_s(4, 0, 128)
+        q2(3)
+        t_x(7, 0)
         c_x(6, 0)
         q1(5)
-        t_x(7, 0)
-        rg_v(3, 256, 512)
-        c_x(6, 1)
+        rg_v(4, 128, 512)
         t_x(7, 1)
+        c_x(6, 1)
         c_x(7, 0)
-        q1(6)
         m1(0)
+        q1(6)
         c_x(7, 1)
-        q2(3)
         m1(1)
-        rg_s(4, 0, 384)
-        q1(7)
+        q2(4)
+        rg_s(5, 0, 512)
         m1(2)
-        row_max(0)
+        q1(7)
+        window()
         m1(3)
-        row_max(1)
+        row_max(0)
         m1(4)
-        expo(0)
-        row_max(2)
+        rg_g(6, 0, 256)
+        row_max(1)
         m1(5)
+        row_max(2)
+        expo(0)
         row_max(3)
+        rg_g(6, 256, 512)
+        row_max(4)
         m1(6)
         expo(1)
-        row_max(4)
-        m1(7)
-        expo(2)
         row_max(5)
         row_max(6)
-        expo(3)
+        m1(7)
+        rg_g(7, 0, 256)
+        expo(2)
         row_max(7)
         rcp(0)
+        expo(3)
         nrm(0)
-        expo(4)
         rcp(1)
         nrm(1)
+        expo(4)
         rcp(2)
-        nrm(2)
-        expo(5)
-        rcp(3)
         colsum(0)
+        nrm(2)
+        rcp(3)
+        expo(5)
+        colsum(1)
         nrm(3)
         rcp(4)
-        colsum(1)
+        colsum(2)
         nrm(4)
-        expo(6)
         rcp(5)
+        expo(6)
+        colsum(3)
         nrm(5)
         rcp(6)
-        colsum(2)
+        colsum(4)
         nrm(6)
         expo(7)
-        colsum(3)
         cast(0)
-        rcp(7)
-        rg_s(4, 384, 512)
-        nrm(7)
-        colsum(4)
-        cast(1)
-        rg_s(5, 0, 512)
-        q3(0)
-        cast(2)
         colsum(5)
-        q3(1)
-        cast(3)
-        q3(2)
+        rcp(7)
+        cast_s(1)
+        nrm(7)
         colsum(6)
+        cast_s(2)
+        q3(0)
+        q3(1)
+        cast_s(3)
         cast(4)
-        q3(3)
         colsum(7)
-        cast(5)
+        q3(2)
+        q3(3)
+        cast_s(5)
         q3(4)
-        rg_s(6, 0, 512)
-        col_recip()
         m2(0)
         cast(6)
-        q3(5)
+        cast_s(7)
+        col_recip()
         m2(1)
-        cast(7)
+        q3(5)
         q3(6)
-        m2(2)
-        q2(4)
+        rg_s(7, 256, 512)
         q3(7)
-        m2(3)
-        rg_v(7, 384, 512)
-        rg_s(7, 0, 384)
-        m2(4)
+        m2(2)
         q2(5)
+        m2(3)
         q2(6)
+        m2(4)
+        q2(7)
         m2(5)
         m2(6)
-        q2(7)
         m2(7)
 
         nc.vector.tensor_scalar_mul(out=o_sb[:], in0=acc[:], scalar1=rcs[:, 0:1])

@@ -13,12 +13,23 @@ ALU = mybir.AluOpType
 AX = mybir.AxisListType
 
 P = 128
+PACK = 4
 N_ROWS = 4096
 D = 512
 K = 128
 BETA = 5.0
-PACK = 4
 G = N_ROWS // (P * PACK)
+
+ROTATING_BANKS = 6
+
+QUARTER = D // 4
+STAGE1_GROUPS = 5
+SCALAR_HELPS = 4
+SCALAR_GROUP = 5
+GPSIMD_PIECES = ((6, 0, D // 2), (6, D // 2, D), (7, 0, D // 2))
+SCALAR_LAST_PIECE = (7, D // 2, D)
+
+VECTOR_CASTS = 3
 
 FLOPS = 2 * 2 * N_ROWS * D * K
 
@@ -27,307 +38,190 @@ def tile_clusternet_pa_kernel(tc, xn, mu, out):
     nc = tc.nc
     with ExitStack() as ctx:
         keep = ctx.enter_context(tc.tile_pool(name="keep", bufs=1))
-        ps_b = ctx.enter_context(tc.psum_pool(name="ps_b", bufs=6))
-        ps_o = ctx.enter_context(tc.psum_pool(name="ps_o", bufs=1))
+        rotating = ctx.enter_context(tc.psum_pool(name="rotating", bufs=ROTATING_BANKS))
+        sums_pool = ctx.enter_context(tc.psum_pool(name="sums_pool", bufs=1))
 
         x_sb = keep.tile([P, G, PACK, D], BF16, name="x_sb")
         mu_sb = keep.tile([P, D], BF16, name="mu_sb")
         ident = keep.tile([P, P], F32, name="ident")
-        xt_grp = keep.tile([P, G, PACK * P, PACK], BF16, name="xt_grp", align_bytes=64)
+        xt_grouped = keep.tile([P, G, PACK * P, PACK], BF16, name="xt_grouped", align_bytes=64)
         xt_codes = keep.tile([P, G, PACK * P], U32, name="xt_codes", align_bytes=64)
         xt_scales = keep.tile([P, G, PACK * P], U8, name="xt_scales", align_bytes=64)
-        mu_grp = keep.tile([P, K, PACK], BF16, name="mu_grp", align_bytes=64)
+        mu_grouped = keep.tile([P, K, PACK], BF16, name="mu_grouped", align_bytes=64)
         mu_codes = keep.tile([P, K], U32, name="mu_codes", align_bytes=64)
         mu_scales = keep.tile([P, K], U8, name="mu_scales", align_bytes=64)
-        xg = keep.tile([P, G, D, PACK], BF16, name="xg", align_bytes=64)
-        x2_codes = keep.tile([P, G, D], U32, name="x2_codes", align_bytes=64)
-        x2_scales = keep.tile([P, G, D], U8, name="x2_scales", align_bytes=64)
+        x_grouped = keep.tile([P, G, D, PACK], BF16, name="x_grouped", align_bytes=64)
+        x_codes = keep.tile([P, G, D], U32, name="x_codes", align_bytes=64)
+        x_scales = keep.tile([P, G, D], U8, name="x_scales", align_bytes=64)
         e_sb = keep.tile([P, G, PACK, K], F32, name="e_sb")
-        r32 = keep.tile([P, G, PACK, K], F32, name="r32")
-        r_sb = keep.tile([P, G, K, PACK], BF16, name="r_sb", align_bytes=64)
+        r_f32 = keep.tile([P, G, PACK, K], F32, name="r_f32")
+        r_grouped = keep.tile([P, G, K, PACK], BF16, name="r_grouped", align_bytes=64)
         r_codes = keep.tile([P, G, K], U32, name="r_codes", align_bytes=64)
         r_scales = keep.tile([P, G, K], U8, name="r_scales", align_bytes=64)
-        mx = keep.tile([P, G, PACK], F32, name="mx")
-        nb = keep.tile([P, G, PACK], F32, name="nb")
-        sums = keep.tile([P, G, PACK], F32, name="sums")
-        rsum = keep.tile([P, G, PACK], F32, name="rsum")
-        warm_in = keep.tile([P, 1], F32, name="warm_in")
-        warm_out = keep.tile([P, 1], F32, name="warm_out")
-        anchor = keep.tile([P, 2], F32, name="anchor")
-        cs_sb = keep.tile([P, 1], F32, name="cs_sb")
-        rcs = keep.tile([P, 1], F32, name="rcs")
-        o_sb = keep.tile([P, D], F32, name="o_sb")
+        row_maxima = keep.tile([P, G, PACK], F32, name="row_maxima")
+        exp_bias = keep.tile([P, G, PACK], F32, name="exp_bias")
+        row_sums = keep.tile([P, G, PACK], F32, name="row_sums")
+        row_recip = keep.tile([P, G, PACK], F32, name="row_recip")
+        table_in = keep.tile([P, 1], F32, name="table_in")
+        table_out = keep.tile([P, 1], F32, name="table_out")
+        one_zero = keep.tile([P, 2], F32, name="one_zero")
+        col_sums = keep.tile([P, 1], F32, name="col_sums")
+        col_recip = keep.tile([P, 1], F32, name="col_recip")
+        out_sb = keep.tile([P, D], F32, name="out_sb")
 
-        acc = ps_o.tile([P, D], F32, name="acc")
-        st = ps_o.tile([P, P], F32, name="st")
+        acc = sums_pool.tile([P, D], F32, name="acc")
+        r_transposed = sums_pool.tile([P, P], F32, name="r_transposed")
 
         banks = {}
 
-        def load_x(g, j0, j1):
-            src = xn[g * P * PACK:(g + 1) * P * PACK, :].rearrange("(p j) d -> p j d", j=PACK)
-            nc.sync.dma_start(out=x_sb[:, g, j0:j1, :], in_=src[:, j0:j1, :])
+        def load_rows(g, j0, j1):
+            rows = xn[g * P * PACK:(g + 1) * P * PACK, :].rearrange("(p j) d -> p j d", j=PACK)
+            nc.sync.dma_start(out=x_sb[:, g, j0:j1, :], in_=rows[:, j0:j1, :])
 
-        def words_out(dst_bf16, bank, cols):
-            dst = dst_bf16.rearrange("p c t -> p (c t)").bitcast(F32).rearrange("p (c u) -> p c u", u=2)
-            nc.scalar.copy(out=dst, in_=bank[:, :, 0:cols].rearrange("p u c -> p c u"))
-
-        def t_mu():
-            tp = ps_b.tile([P, 2, 2 * P], F32, name="tp", tag="bank")
-            banks["mu"] = tp
+        def transpose_words(bank, column, bf16_rows):
+            words = bf16_rows.bitcast(F32)
             for u in range(2):
-                nc.tensor.transpose(tp[:, u, 0:P], mu_sb[:].bitcast(F32)[:, u * P:(u + 1) * P], ident[:])
+                nc.tensor.transpose(bank[:, u, column:column + P], words[:, u * P:(u + 1) * P], ident[:])
 
-        def c_mu():
-            words_out(mu_grp[:, :, :], banks["mu"], P)
+        def copy_words_out(grouped, bank, columns):
+            dst = grouped.rearrange("p c t -> p (c t)").bitcast(F32).rearrange("p (c u) -> p c u", u=2)
+            nc.scalar.copy(out=dst, in_=bank[:, :, 0:columns].rearrange("p u c -> p c u"))
 
-        def q_mu():
-            nc.vector.quantize_mx(out=mu_codes[:].bitcast(FP8X4), scales=mu_scales[:],
-                                  in_=mu_grp[:].rearrange("p c t -> p (c t)"))
+        def quantise(codes, scales, grouped):
+            nc.vector.quantize_mx(out=codes.bitcast(FP8X4), scales=scales, in_=grouped)
 
-        def t_x(g, h):
-            tp = ps_b.tile([P, 2, 2 * P], F32, name="tp", tag="bank")
-            banks[(g, h)] = tp
-            for jj in range(2):
-                xw = x_sb[:, g, 2 * h + jj, :].bitcast(F32)
-                for u in range(2):
-                    nc.tensor.transpose(tp[:, u, jj * P:(jj + 1) * P], xw[:, u * P:(u + 1) * P], ident[:])
+        def transpose_group(g):
+            for h in range(2):
+                bank = rotating.tile([P, 2, 2 * P], F32, name="bank", tag="bank")
+                banks[("xt", g, h)] = bank
+                for i in range(2):
+                    transpose_words(bank, i * P, x_sb[:, g, 2 * h + i, :])
 
-        def c_x(g, h):
-            words_out(xt_grp[:, g, 2 * h * P:(2 * h + 2) * P, :], banks[(g, h)], 2 * P)
+        def copy_group_out(g):
+            for h in range(2):
+                copy_words_out(xt_grouped[:, g, 2 * h * P:(2 * h + 2) * P, :], banks[("xt", g, h)], 2 * P)
 
-        def q1(g):
-            nc.vector.quantize_mx(out=xt_codes[:, g, :].bitcast(FP8X4), scales=xt_scales[:, g, :],
-                                  in_=xt_grp[:, g, :, :].rearrange("p c t -> p (c t)"))
+        def quantise_features(g):
+            quantise(xt_codes[:, g, :], xt_scales[:, g, :], xt_grouped[:, g, :, :].rearrange("p c t -> p (c t)"))
 
-        def m1(g):
-            lg = ps_b.tile([P, PACK, K], F32, name="lg", tag="bank")
-            banks[("l", g)] = lg
+        def regroup(copy, g, d0, d1):
+            copy(out=x_grouped[:, g, d0:d1, :].rearrange("p (c i) j -> p c j i", i=4),
+                 in_=x_sb[:, g, :, d0:d1].rearrange("p j (c i) -> p c j i", i=4))
+
+        def regroup_on_gpsimd(g, d0, d1):
+            nc.gpsimd.tensor_scalar(out=x_grouped[:, g, d0:d1, :],
+                                    in0=x_sb[:, g, :, d0:d1].rearrange("p j d -> p d j"),
+                                    scalar1=one_zero[:, 0:1], scalar2=one_zero[:, 1:2],
+                                    op0=ALU.mult, op1=ALU.add)
+
+        def quantise_rows(g):
+            quantise(x_codes[:, g, :], x_scales[:, g, :], x_grouped[:, g, :, :].rearrange("p d j -> p (d j)"))
+
+        def first_matmul(g):
+            logits = rotating.tile([P, PACK, K], F32, name="logits", tag="bank")
+            banks[("logits", g)] = logits
             for j in range(PACK):
-                nc.tensor.matmul_mx(out=lg[:, j, :],
+                nc.tensor.matmul_mx(out=logits[:, j, :],
                                     lhsT=xt_codes[:, g, j * P:(j + 1) * P].bitcast(FP8X4),
                                     lhsT_scale=xt_scales[:, g, j * P:(j + 1) * P],
                                     rhs=mu_codes[:].bitcast(FP8X4), rhs_scale=mu_scales[:],
                                     start=True, stop=True)
 
-        def window():
-            nc.vector.memset(anchor[:, 0:1], 1.0)
-            nc.vector.memset(anchor[:, 1:2], 0.0)
+        def row_maximum(g):
+            nc.vector.tensor_reduce(out=row_maxima[:, g, :], in_=banks[("logits", g)][:], axis=AX.X, op=ALU.max)
 
-        def row_max(g):
-            nc.vector.tensor_reduce(out=mx[:, g, :], in_=banks[("l", g)][:], axis=AX.X, op=ALU.max)
-
-        def expo(g):
-            lg = banks[("l", g)]
-            nc.scalar.mul(nb[:, g, :], mx[:, g, :], -BETA)
+        def exponentials(g):
+            logits = banks[("logits", g)]
+            nc.scalar.mul(exp_bias[:, g, :], row_maxima[:, g, :], -BETA)
             for j in range(PACK):
-                nc.scalar.activation(out=e_sb[:, g, j, :], in_=lg[:, j, :], func=AF.Exp,
-                                     bias=nb[:, g, j:j + 1], scale=BETA, accum_out=sums[:, g, j:j + 1])
+                nc.scalar.activation(out=e_sb[:, g, j, :], in_=logits[:, j, :], func=AF.Exp,
+                                     bias=exp_bias[:, g, j:j + 1], scale=BETA,
+                                     accum_out=row_sums[:, g, j:j + 1])
 
-        def rcp(g):
-            nc.vector.reciprocal(rsum[:, g, :], sums[:, g, :])
-
-        def nrm(g):
+        def normalise(g):
+            nc.vector.reciprocal(row_recip[:, g, :], row_sums[:, g, :])
             for j in range(PACK):
-                nc.vector.tensor_scalar_mul(out=r32[:, g, j, :], in0=e_sb[:, g, j, :], scalar1=rsum[:, g, j:j + 1])
+                nc.vector.tensor_scalar_mul(out=r_f32[:, g, j, :], in0=e_sb[:, g, j, :],
+                                            scalar1=row_recip[:, g, j:j + 1])
 
-        def cast(g):
-            nc.vector.tensor_copy(out=r_sb[:, g, :, :], in_=r32[:, g, :, :].rearrange("p j k -> p k j"))
-
-        def cast_s(g):
-            nc.scalar.copy(out=r_sb[:, g, :, :], in_=r32[:, g, :, :].rearrange("p j k -> p k j"))
-
-        def colsum(g):
+        def add_to_colsum(g):
             for j in range(PACK):
-                nc.tensor.matmul(out=st[:], lhsT=r32[:, g, j, :], rhs=ident[:], is_transpose=True,
+                nc.tensor.matmul(out=r_transposed[:], lhsT=r_f32[:, g, j, :], rhs=ident[:], is_transpose=True,
                                  start=(g == 0 and j == 0), stop=(g == G - 1 and j == PACK - 1))
 
-        def col_recip():
-            nc.vector.tensor_reduce(out=cs_sb[:], in_=st[:], axis=AX.X, op=ALU.add)
-            nc.vector.reciprocal(rcs[:], cs_sb[:])
+        def cast_r(copy, g):
+            copy(out=r_grouped[:, g, :, :], in_=r_f32[:, g, :, :].rearrange("p j k -> p k j"))
 
-        def q3(g):
-            nc.vector.quantize_mx(out=r_codes[:, g, :].bitcast(FP8X4), scales=r_scales[:, g, :],
-                                  in_=r_sb[:, g, :, :].rearrange("p k j -> p (k j)"))
+        def quantise_r(g):
+            quantise(r_codes[:, g, :], r_scales[:, g, :], r_grouped[:, g, :, :].rearrange("p k j -> p (k j)"))
 
-        def regroup(engine_copy, g, d0, d1):
-            engine_copy(out=xg[:, g, d0:d1, :].rearrange("p (c i) t -> p c t i", i=4),
-                        in_=x_sb[:, g, :, d0:d1].rearrange("p t (c i) -> p c t i", i=4))
-
-        def rg_s(g, d0, d1):
-            regroup(nc.scalar.copy, g, d0, d1)
-
-        def rg_v(g, d0, d1):
-            regroup(nc.vector.tensor_copy, g, d0, d1)
-
-        def rg_g(g, d0, d1):
-            nc.gpsimd.tensor_scalar(out=xg[:, g, d0:d1, :], in0=x_sb[:, g, :, d0:d1].rearrange("p t d -> p d t"),
-                                    scalar1=anchor[:, 0:1], scalar2=anchor[:, 1:2], op0=ALU.mult, op1=ALU.add)
-
-        def q2(g):
-            nc.vector.quantize_mx(out=x2_codes[:, g, :].bitcast(FP8X4), scales=x2_scales[:, g, :],
-                                  in_=xg[:, g, :, :].rearrange("p d j -> p (d j)"))
-
-        def m2(g):
+        def second_matmul(g):
             nc.tensor.matmul_mx(out=acc[:], lhsT=r_codes[:, g, :].bitcast(FP8X4), lhsT_scale=r_scales[:, g, :],
-                                rhs=x2_codes[:, g, :].bitcast(FP8X4), rhs_scale=x2_scales[:, g, :],
+                                rhs=x_codes[:, g, :].bitcast(FP8X4), rhs_scale=x_scales[:, g, :],
                                 start=(g == 0), stop=(g == G - 1))
 
         ctx.enter_context(tc.manual_schedule())
 
         nc.scalar.dma_start(out=mu_sb[:], in_=mu[:, :])
-        load_x(0, 0, 2)
-        load_x(0, 2, 4)
+        load_rows(0, 0, PACK // 2)
+        load_rows(0, PACK // 2, PACK)
         for g in range(1, G):
-            load_x(g, 0, PACK)
+            load_rows(g, 0, PACK)
         make_identity(nc, ident[:])
-        nc.vector.memset(warm_in[:], 0.0)
-        nc.scalar.activation(out=warm_out[:], in_=warm_in[:], func=AF.Exp)
+        nc.vector.memset(table_in[:], 0.0)
+        nc.scalar.activation(out=table_out[:], in_=table_in[:], func=AF.Exp)
 
-        t_mu()
-        t_x(0, 0)
-        c_mu()
-        rg_v(0, 128, 384)
-        t_x(0, 1)
-        q_mu()
-        rg_s(0, 0, 128)
-        rg_v(0, 384, 512)
-        c_x(0, 0)
-        rg_v(1, 128, 256)
-        t_x(1, 0)
-        c_x(0, 1)
-        q2(0)
-        rg_v(1, 256, 384)
-        t_x(1, 1)
-        rg_s(1, 0, 128)
-        q1(0)
-        c_x(1, 0)
-        t_x(2, 0)
-        rg_v(1, 384, 512)
-        rg_v(2, 128, 256)
-        c_x(1, 1)
-        t_x(2, 1)
-        q2(1)
-        c_x(2, 0)
-        t_x(3, 0)
-        q1(1)
-        rg_s(2, 0, 128)
-        rg_v(2, 256, 512)
-        t_x(3, 1)
-        c_x(2, 1)
-        rg_v(3, 0, 128)
-        t_x(4, 0)
-        c_x(3, 0)
-        q2(2)
-        t_x(4, 1)
-        c_x(3, 1)
-        q1(2)
-        c_x(4, 0)
-        t_x(5, 0)
-        rg_v(3, 128, 256)
-        c_x(4, 1)
-        q1(3)
-        t_x(5, 1)
-        rg_v(3, 256, 512)
-        c_x(5, 0)
-        t_x(6, 0)
-        c_x(5, 1)
-        q1(4)
-        t_x(6, 1)
-        rg_s(4, 0, 128)
-        q2(3)
-        t_x(7, 0)
-        c_x(6, 0)
-        q1(5)
-        rg_v(4, 128, 512)
-        t_x(7, 1)
-        c_x(6, 1)
-        c_x(7, 0)
-        m1(0)
-        q1(6)
-        c_x(7, 1)
-        m1(1)
-        q2(4)
-        rg_s(5, 0, 512)
-        m1(2)
-        q1(7)
-        window()
-        m1(3)
-        row_max(0)
-        m1(4)
-        rg_g(6, 0, 256)
-        row_max(1)
-        m1(5)
-        row_max(2)
-        expo(0)
-        row_max(3)
-        rg_g(6, 256, 512)
-        row_max(4)
-        m1(6)
-        expo(1)
-        row_max(5)
-        row_max(6)
-        m1(7)
-        rg_g(7, 0, 256)
-        expo(2)
-        row_max(7)
-        rcp(0)
-        expo(3)
-        nrm(0)
-        rcp(1)
-        nrm(1)
-        expo(4)
-        rcp(2)
-        colsum(0)
-        nrm(2)
-        rcp(3)
-        expo(5)
-        colsum(1)
-        nrm(3)
-        rcp(4)
-        colsum(2)
-        nrm(4)
-        rcp(5)
-        expo(6)
-        colsum(3)
-        nrm(5)
-        rcp(6)
-        colsum(4)
-        nrm(6)
-        expo(7)
-        cast(0)
-        colsum(5)
-        rcp(7)
-        cast_s(1)
-        nrm(7)
-        colsum(6)
-        cast_s(2)
-        q3(0)
-        q3(1)
-        cast_s(3)
-        cast(4)
-        colsum(7)
-        q3(2)
-        q3(3)
-        cast_s(5)
-        q3(4)
-        m2(0)
-        cast(6)
-        cast_s(7)
-        col_recip()
-        m2(1)
-        q3(5)
-        q3(6)
-        rg_s(7, 256, 512)
-        q3(7)
-        m2(2)
-        q2(5)
-        m2(3)
-        q2(6)
-        m2(4)
-        q2(7)
-        m2(5)
-        m2(6)
-        m2(7)
+        mu_bank = rotating.tile([P, 2, 2 * P], F32, name="bank", tag="bank")
+        transpose_words(mu_bank, 0, mu_sb[:])
+        copy_words_out(mu_grouped[:, :, :], mu_bank, P)
+        for g in range(G + 1):
+            if g < G:
+                transpose_group(g)
+            if 1 <= g <= SCALAR_HELPS:
+                regroup(nc.scalar.copy, g - 1, 0, QUARTER)
+            if g >= 1:
+                copy_group_out(g - 1)
+            if g < STAGE1_GROUPS:
+                regroup(nc.vector.tensor_copy, g, QUARTER if g < SCALAR_HELPS else 0, D)
+            if g == 0:
+                quantise(mu_codes[:], mu_scales[:], mu_grouped[:].rearrange("p c t -> p (c t)"))
+            if 1 <= g <= STAGE1_GROUPS:
+                quantise_rows(g - 1)
+            if g >= 1:
+                quantise_features(g - 1)
 
-        nc.vector.tensor_scalar_mul(out=o_sb[:], in0=acc[:], scalar1=rcs[:, 0:1])
-        nc.sync.dma_start(out=out[:, :], in_=o_sb[:])
+        for g in range(ROTATING_BANKS):
+            first_matmul(g)
+        regroup(nc.scalar.copy, SCALAR_GROUP, 0, D)
+        nc.vector.memset(one_zero[:, 0:1], 1.0)
+        nc.vector.memset(one_zero[:, 1:2], 0.0)
+        for piece in GPSIMD_PIECES:
+            regroup_on_gpsimd(*piece)
+        for g in range(G):
+            row_maximum(g)
+            exponentials(g)
+            if g + ROTATING_BANKS < G:
+                first_matmul(g + ROTATING_BANKS)
+
+        for g in range(G):
+            if g == G - 1:
+                cast_r(nc.vector.tensor_copy, 0)
+            normalise(g)
+            add_to_colsum(g)
+        for g in range(VECTOR_CASTS, G):
+            cast_r(nc.scalar.copy, g)
+        regroup(nc.scalar.copy, *SCALAR_LAST_PIECE)
+        for g in range(1, VECTOR_CASTS):
+            cast_r(nc.vector.tensor_copy, g)
+            quantise_r(g - 1)
+        nc.vector.tensor_reduce(out=col_sums[:], in_=r_transposed[:], axis=AX.X, op=ALU.add)
+        nc.vector.reciprocal(col_recip[:], col_sums[:])
+        for g in range(VECTOR_CASTS - 1, G):
+            quantise_r(g)
+        for g in range(STAGE1_GROUPS, G):
+            quantise_rows(g)
+        for g in range(G):
+            second_matmul(g)
+
+        nc.vector.tensor_scalar_mul(out=out_sb[:], in0=acc[:], scalar1=col_recip[:, 0:1])
+        nc.sync.dma_start(out=out[:, :], in_=out_sb[:])

@@ -23,11 +23,12 @@ G = N_ROWS // (P * PACK)
 ROTATING_BANKS = 6
 
 QUARTER = D // 4
+HALF = D // 2
 STAGE1_GROUPS = 5
 SCALAR_HELPS = 4
 SCALAR_GROUP = 5
-GPSIMD_PIECES = ((6, 0, D // 2), (6, D // 2, D), (7, 0, D // 2))
-SCALAR_LAST_PIECE = (7, D // 2, D)
+GPSIMD_PIECES = ((6, 0, HALF), (6, HALF, D), (7, 0, HALF))
+SCALAR_LAST_PIECE = (7, HALF, D)
 
 VECTOR_CASTS = 3
 
@@ -69,8 +70,7 @@ def tile_clusternet_pa_kernel(tc, xn, mu, out):
         col_recip = keep.tile([P, 1], F32, name="col_recip")
         out_sb = keep.tile([P, D], F32, name="out_sb")
 
-        acc = sums_pool.tile([P, D], F32, name="acc")
-        r_transposed = sums_pool.tile([P, P], F32, name="r_transposed")
+        acc = (sums_pool.tile([P, HALF], F32, name="acc_lo"), sums_pool.tile([P, HALF], F32, name="acc_hi"))
 
         banks = {}
 
@@ -114,8 +114,9 @@ def tile_clusternet_pa_kernel(tc, xn, mu, out):
                                     scalar1=one_zero[:, 0:1], scalar2=one_zero[:, 1:2],
                                     op0=ALU.mult, op1=ALU.add)
 
-        def quantise_rows(g):
-            quantise(x_codes[:, g, :], x_scales[:, g, :], x_grouped[:, g, :, :].rearrange("p d j -> p (d j)"))
+        def quantise_rows(g, d0, d1):
+            quantise(x_codes[:, g, d0:d1], x_scales[:, g, d0:d1],
+                     x_grouped[:, g, d0:d1, :].rearrange("p d j -> p (d j)"))
 
         def first_matmul(g):
             logits = rotating.tile([P, PACK, K], F32, name="logits", tag="bank")
@@ -146,7 +147,7 @@ def tile_clusternet_pa_kernel(tc, xn, mu, out):
 
         def add_to_colsum(g):
             for j in range(PACK):
-                nc.tensor.matmul(out=r_transposed[:], lhsT=r_f32[:, g, j, :], rhs=ident[:], is_transpose=True,
+                nc.tensor.matmul(out=banks["colsum"][:], lhsT=r_f32[:, g, j, :], rhs=ident[:], is_transpose=True,
                                  start=(g == 0 and j == 0), stop=(g == G - 1 and j == PACK - 1))
 
         def cast_r(copy, g):
@@ -156,9 +157,12 @@ def tile_clusternet_pa_kernel(tc, xn, mu, out):
             quantise(r_codes[:, g, :], r_scales[:, g, :], r_grouped[:, g, :, :].rearrange("p k j -> p (k j)"))
 
         def second_matmul(g):
-            nc.tensor.matmul_mx(out=acc[:], lhsT=r_codes[:, g, :].bitcast(FP8X4), lhsT_scale=r_scales[:, g, :],
-                                rhs=x_codes[:, g, :].bitcast(FP8X4), rhs_scale=x_scales[:, g, :],
-                                start=(g == 0), stop=(g == G - 1))
+            for half in range(2):
+                nc.tensor.matmul_mx(out=acc[half][:],
+                                    lhsT=r_codes[:, g, :].bitcast(FP8X4), lhsT_scale=r_scales[:, g, :],
+                                    rhs=x_codes[:, g, half * HALF:(half + 1) * HALF].bitcast(FP8X4),
+                                    rhs_scale=x_scales[:, g, half * HALF:(half + 1) * HALF],
+                                    start=(g == 0), stop=(g == G - 1))
 
         ctx.enter_context(tc.manual_schedule())
 
@@ -186,7 +190,7 @@ def tile_clusternet_pa_kernel(tc, xn, mu, out):
             if g == 0:
                 quantise(mu_codes[:], mu_scales[:], mu_grouped[:].rearrange("p c t -> p (c t)"))
             if 1 <= g <= STAGE1_GROUPS:
-                quantise_rows(g - 1)
+                quantise_rows(g - 1, 0, D)
             if g >= 1:
                 quantise_features(g - 1)
 
@@ -203,6 +207,7 @@ def tile_clusternet_pa_kernel(tc, xn, mu, out):
             if g + ROTATING_BANKS < G:
                 first_matmul(g + ROTATING_BANKS)
 
+        banks["colsum"] = rotating.tile([P, P], F32, name="r_transposed", tag="bank")
         for g in range(G):
             if g == G - 1:
                 cast_r(nc.vector.tensor_copy, 0)
@@ -214,14 +219,18 @@ def tile_clusternet_pa_kernel(tc, xn, mu, out):
         for g in range(1, VECTOR_CASTS):
             cast_r(nc.vector.tensor_copy, g)
             quantise_r(g - 1)
-        nc.vector.tensor_reduce(out=col_sums[:], in_=r_transposed[:], axis=AX.X, op=ALU.add)
+        nc.vector.tensor_reduce(out=col_sums[:], in_=banks["colsum"][:], axis=AX.X, op=ALU.add)
         nc.vector.reciprocal(col_recip[:], col_sums[:])
         for g in range(VECTOR_CASTS - 1, G):
             quantise_r(g)
-        for g in range(STAGE1_GROUPS, G):
-            quantise_rows(g)
+        for g in range(STAGE1_GROUPS, G - 1):
+            quantise_rows(g, 0, D)
+        quantise_rows(G - 1, 0, HALF)
+        quantise_rows(G - 1, HALF, D)
         for g in range(G):
             second_matmul(g)
 
-        nc.vector.tensor_scalar_mul(out=out_sb[:], in0=acc[:], scalar1=col_recip[:, 0:1])
-        nc.sync.dma_start(out=out[:, :], in_=out_sb[:])
+        nc.scalar.activation(out=out_sb[:, 0:HALF], in_=acc[0][:], func=AF.Copy, scale=col_recip[:, 0:1])
+        nc.sync.dma_start(out=out[:, 0:HALF], in_=out_sb[:, 0:HALF])
+        nc.vector.tensor_scalar_mul(out=out_sb[:, HALF:D], in0=acc[1][:], scalar1=col_recip[:, 0:1])
+        nc.sync.dma_start(out=out[:, HALF:D], in_=out_sb[:, HALF:D])

@@ -20,7 +20,7 @@ K = 128
 BETA = 5.0
 G = N_ROWS // (P * PACK)
 
-ROTATING_BANKS = 6
+BANKS = 8
 
 QUARTER = D // 4
 HALF = D // 2
@@ -32,6 +32,8 @@ SCALAR_LAST_PIECE = (7, HALF, D)
 
 VECTOR_CASTS = 3
 
+BIASES_BEHIND = {0: (2, 3), 1: (3, 5), 3: (5, 8)}
+
 FLOPS = 2 * 2 * N_ROWS * D * K
 
 
@@ -39,8 +41,7 @@ def tile_clusternet_pa_kernel(tc, xn, mu, out):
     nc = tc.nc
     with ExitStack() as ctx:
         keep = ctx.enter_context(tc.tile_pool(name="keep", bufs=1))
-        rotating = ctx.enter_context(tc.psum_pool(name="rotating", bufs=ROTATING_BANKS))
-        sums_pool = ctx.enter_context(tc.psum_pool(name="sums_pool", bufs=1))
+        rotating = ctx.enter_context(tc.psum_pool(name="rotating", bufs=BANKS))
 
         x_sb = keep.tile([P, G, PACK, D], BF16, name="x_sb")
         mu_sb = keep.tile([P, D], BF16, name="mu_sb")
@@ -69,8 +70,6 @@ def tile_clusternet_pa_kernel(tc, xn, mu, out):
         col_sums = keep.tile([P, 1], F32, name="col_sums")
         col_recip = keep.tile([P, 1], F32, name="col_recip")
         out_sb = keep.tile([P, D], F32, name="out_sb")
-
-        acc = (sums_pool.tile([P, HALF], F32, name="acc_lo"), sums_pool.tile([P, HALF], F32, name="acc_hi"))
 
         banks = {}
 
@@ -131,16 +130,20 @@ def tile_clusternet_pa_kernel(tc, xn, mu, out):
         def row_maximum(g):
             nc.vector.tensor_reduce(out=row_maxima[:, g, :], in_=banks[("logits", g)][:], axis=AX.X, op=ALU.max)
 
+        def bias(g0, g1):
+            nc.scalar.mul(exp_bias[:, g0:g1, :], row_maxima[:, g0:g1, :], -BETA)
+
         def exponentials(g):
             logits = banks[("logits", g)]
-            nc.scalar.mul(exp_bias[:, g, :], row_maxima[:, g, :], -BETA)
             for j in range(PACK):
                 nc.scalar.activation(out=e_sb[:, g, j, :], in_=logits[:, j, :], func=AF.Exp,
                                      bias=exp_bias[:, g, j:j + 1], scale=BETA,
                                      accum_out=row_sums[:, g, j:j + 1])
 
+        def reciprocals(g0, g1):
+            nc.vector.reciprocal(row_recip[:, g0:g1, :], row_sums[:, g0:g1, :])
+
         def normalise(g):
-            nc.vector.reciprocal(row_recip[:, g, :], row_sums[:, g, :])
             for j in range(PACK):
                 nc.vector.tensor_scalar_mul(out=r_f32[:, g, j, :], in0=e_sb[:, g, j, :],
                                             scalar1=row_recip[:, g, j:j + 1])
@@ -158,7 +161,7 @@ def tile_clusternet_pa_kernel(tc, xn, mu, out):
 
         def second_matmul(g):
             for half in range(2):
-                nc.tensor.matmul_mx(out=acc[half][:],
+                nc.tensor.matmul_mx(out=banks[("acc", half)][:],
                                     lhsT=r_codes[:, g, :].bitcast(FP8X4), lhsT_scale=r_scales[:, g, :],
                                     rhs=x_codes[:, g, half * HALF:(half + 1) * HALF].bitcast(FP8X4),
                                     rhs_scale=x_scales[:, g, half * HALF:(half + 1) * HALF],
@@ -194,43 +197,62 @@ def tile_clusternet_pa_kernel(tc, xn, mu, out):
             if g >= 1:
                 quantise_features(g - 1)
 
-        for g in range(ROTATING_BANKS):
+        for g in range(G):
             first_matmul(g)
-        regroup(nc.scalar.copy, SCALAR_GROUP, 0, D)
         nc.vector.memset(one_zero[:, 0:1], 1.0)
         nc.vector.memset(one_zero[:, 1:2], 0.0)
         for piece in GPSIMD_PIECES:
             regroup_on_gpsimd(*piece)
         for g in range(G):
             row_maximum(g)
+        regroup(nc.scalar.copy, SCALAR_GROUP, 0, 3 * QUARTER)
+        bias(0, 1)
+        regroup(nc.scalar.copy, SCALAR_GROUP, 3 * QUARTER, D)
+        bias(1, 2)
+        for g in range(G):
             exponentials(g)
-            if g + ROTATING_BANKS < G:
-                first_matmul(g + ROTATING_BANKS)
+            if g in BIASES_BEHIND:
+                bias(*BIASES_BEHIND[g])
 
         banks["colsum"] = rotating.tile([P, P], F32, name="r_transposed", tag="bank")
+        reciprocals(0, 2)
+        quantise_rows(5, 0, D)
+        normalise(0)
+        normalise(1)
+        reciprocals(2, 4)
+        quantise_rows(6, 0, D)
+        normalise(2)
+        normalise(3)
+        reciprocals(4, 6)
+        cast_r(nc.vector.tensor_copy, 0)
+        quantise_rows(7, 0, HALF)
+        normalise(4)
+        normalise(5)
+        reciprocals(6, 8)
+        cast_r(nc.vector.tensor_copy, 1)
+        quantise_r(0)
+        normalise(6)
+        normalise(7)
+        cast_r(nc.vector.tensor_copy, 2)
         for g in range(G):
-            if g == G - 1:
-                cast_r(nc.vector.tensor_copy, 0)
-            normalise(g)
             add_to_colsum(g)
         for g in range(VECTOR_CASTS, G):
             cast_r(nc.scalar.copy, g)
         regroup(nc.scalar.copy, *SCALAR_LAST_PIECE)
-        for g in range(1, VECTOR_CASTS):
-            cast_r(nc.vector.tensor_copy, g)
-            quantise_r(g - 1)
+        quantise_r(1)
+        quantise_r(2)
         nc.vector.tensor_reduce(out=col_sums[:], in_=banks["colsum"][:], axis=AX.X, op=ALU.add)
+        quantise_r(3)
         nc.vector.reciprocal(col_recip[:], col_sums[:])
-        for g in range(VECTOR_CASTS - 1, G):
+        for g in range(4, G):
             quantise_r(g)
-        for g in range(STAGE1_GROUPS, G - 1):
-            quantise_rows(g, 0, D)
-        quantise_rows(G - 1, 0, HALF)
         quantise_rows(G - 1, HALF, D)
+        for half in range(2):
+            banks[("acc", half)] = rotating.tile([P, HALF], F32, name="acc", tag="bank")
         for g in range(G):
             second_matmul(g)
 
-        nc.scalar.activation(out=out_sb[:, 0:HALF], in_=acc[0][:], func=AF.Copy, scale=col_recip[:, 0:1])
+        nc.scalar.activation(out=out_sb[:, 0:HALF], in_=banks[("acc", 0)][:], func=AF.Copy, scale=col_recip[:, 0:1])
         nc.sync.dma_start(out=out[:, 0:HALF], in_=out_sb[:, 0:HALF])
-        nc.vector.tensor_scalar_mul(out=out_sb[:, HALF:D], in0=acc[1][:], scalar1=col_recip[:, 0:1])
+        nc.vector.tensor_scalar_mul(out=out_sb[:, HALF:D], in0=banks[("acc", 1)][:], scalar1=col_recip[:, 0:1])
         nc.sync.dma_start(out=out[:, HALF:D], in_=out_sb[:, HALF:D])

@@ -215,41 +215,51 @@ def tile_clusternet_pa_kernel(tc, xn, mu, out):
                 bias(*BIASES_BEHIND[g])
 
         banks["colsum"] = rotating.tile([P, P], F32, name="r_transposed", tag="bank")
+        for half in range(2):
+            banks[("acc", half)] = rotating.tile([P, HALF], F32, name="acc", tag="bank")
+
         reciprocals(0, 2)
         quantise_rows(5, 0, D)
         normalise(0)
         normalise(1)
         reciprocals(2, 4)
-        quantise_rows(6, 0, D)
+        cast_r(nc.vector.tensor_copy, 0)
+        cast_r(nc.vector.tensor_copy, 1)
         normalise(2)
         normalise(3)
         reciprocals(4, 6)
-        cast_r(nc.vector.tensor_copy, 0)
-        quantise_rows(7, 0, HALF)
+        quantise_r(0)
+        quantise_r(1)
+        cast_r(nc.vector.tensor_copy, 2)
         normalise(4)
         normalise(5)
         reciprocals(6, 8)
-        cast_r(nc.vector.tensor_copy, 1)
-        quantise_r(0)
+        quantise_r(2)
+        quantise_rows(6, 0, D)
         normalise(6)
         normalise(7)
-        cast_r(nc.vector.tensor_copy, 2)
-        for g in range(G):
-            add_to_colsum(g)
+        quantise_rows(7, 0, HALF)
+        regroup(nc.scalar.copy, *SCALAR_LAST_PIECE)
         for g in range(VECTOR_CASTS, G):
             cast_r(nc.scalar.copy, g)
-        regroup(nc.scalar.copy, *SCALAR_LAST_PIECE)
-        quantise_r(1)
-        quantise_r(2)
-        nc.vector.tensor_reduce(out=col_sums[:], in_=banks["colsum"][:], axis=AX.X, op=ALU.add)
+        for g in range(4):
+            add_to_colsum(g)
+        second_matmul(0)
+        second_matmul(1)
+        add_to_colsum(4)
+        add_to_colsum(5)
+        second_matmul(2)
+        add_to_colsum(6)
+        add_to_colsum(7)
         quantise_r(3)
+        quantise_r(4)
+        quantise_rows(7, HALF, D)
+        quantise_r(5)
+        quantise_r(6)
+        nc.vector.tensor_reduce(out=col_sums[:], in_=banks["colsum"][:], axis=AX.X, op=ALU.add)
+        quantise_r(7)
         nc.vector.reciprocal(col_recip[:], col_sums[:])
-        for g in range(4, G):
-            quantise_r(g)
-        quantise_rows(G - 1, HALF, D)
-        for half in range(2):
-            banks[("acc", half)] = rotating.tile([P, HALF], F32, name="acc", tag="bank")
-        for g in range(G):
+        for g in range(3, G):
             second_matmul(g)
 
         nc.scalar.activation(out=out_sb[:, 0:HALF], in_=banks[("acc", 0)][:], func=AF.Copy, scale=col_recip[:, 0:1])

@@ -34,6 +34,9 @@ VECTOR_CASTS = 3
 
 BIASES_BEHIND = {0: (2, 3), 1: (3, 5), 3: (5, 8)}
 
+WARM_PASSES = 4
+MU_STEP = 2
+
 FLOPS = 2 * 2 * N_ROWS * D * K
 
 
@@ -169,28 +172,31 @@ def tile_clusternet_pa_kernel(tc, xn, mu, out):
 
         ctx.enter_context(tc.manual_schedule())
 
-        nc.scalar.dma_start(out=mu_sb[:], in_=mu[:, :])
         load_rows(0, 0, PACK // 2)
         load_rows(0, PACK // 2, PACK)
         for g in range(1, G):
             load_rows(g, 0, PACK)
+            if g == MU_STEP:
+                nc.sync.dma_start(out=mu_sb[:], in_=mu[:, :])
         make_identity(nc, ident[:])
         nc.vector.memset(table_in[:], 0.0)
         nc.scalar.activation(out=table_out[:], in_=table_in[:], func=AF.Exp)
 
-        mu_bank = rotating.tile([P, 2, 2 * P], F32, name="bank", tag="bank")
-        transpose_words(mu_bank, 0, mu_sb[:])
-        copy_words_out(mu_grouped[:, :, :], mu_bank, P)
         for g in range(G + 1):
             if g < G:
                 transpose_group(g)
+            if g == MU_STEP:
+                mu_bank = rotating.tile([P, 2, 2 * P], F32, name="bank", tag="bank")
+                transpose_words(mu_bank, 0, mu_sb[:])
             if 1 <= g <= SCALAR_HELPS:
                 regroup(nc.scalar.copy, g - 1, 0, QUARTER)
             if g >= 1:
                 copy_group_out(g - 1)
+            if g == MU_STEP + 1:
+                copy_words_out(mu_grouped[:, :, :], mu_bank, P)
             if g < STAGE1_GROUPS:
                 regroup(nc.vector.tensor_copy, g, QUARTER if g < SCALAR_HELPS else 0, D)
-            if g == 0:
+            if g == MU_STEP + 2:
                 quantise(mu_codes[:], mu_scales[:], mu_grouped[:].rearrange("p c t -> p (c t)"))
             if 1 <= g <= STAGE1_GROUPS:
                 quantise_rows(g - 1, 0, D)
@@ -214,6 +220,12 @@ def tile_clusternet_pa_kernel(tc, xn, mu, out):
             if g in BIASES_BEHIND:
                 bias(*BIASES_BEHIND[g])
 
+        for i in range(WARM_PASSES):
+            warm_bank = rotating.tile([P, D], F32, name="warm_bank", tag="bank")
+            nc.tensor.matmul_mx(out=warm_bank[:],
+                                lhsT=x_codes[:, 0, 0:P].bitcast(FP8X4), lhsT_scale=x_scales[:, 0, 0:P],
+                                rhs=x_codes[:, 0, :].bitcast(FP8X4), rhs_scale=x_scales[:, 0, :],
+                                start=True, stop=True)
         banks["colsum"] = rotating.tile([P, P], F32, name="r_transposed", tag="bank")
         for half in range(2):
             banks[("acc", half)] = rotating.tile([P, HALF], F32, name="acc", tag="bank")

@@ -30,7 +30,8 @@ SCALAR_GROUP = 5
 GPSIMD_PIECES = ((6, 0, HALF), (6, HALF, D), (7, 0, HALF))
 SCALAR_LAST_PIECE = (7, HALF, D)
 
-VECTOR_CASTS = 3
+BLOCKS = ((0, HALF), (HALF, 3 * QUARTER), (3 * QUARTER, D))
+LAST_GROUP = (6, 6, 7)
 
 BIASES_BEHIND = {0: (2, 3), 1: (3, 5), 3: (5, 8)}
 
@@ -70,6 +71,7 @@ def tile_clusternet_pa_kernel(tc, xn, mu, out):
         table_in = keep.tile([P, 1], F32, name="table_in")
         table_out = keep.tile([P, 1], F32, name="table_out")
         one_zero = keep.tile([P, 2], F32, name="one_zero")
+        colsum_copy = keep.tile([P, P], F32, name="colsum_copy")
         col_sums = keep.tile([P, 1], F32, name="col_sums")
         col_recip = keep.tile([P, 1], F32, name="col_recip")
         out_sb = keep.tile([P, D], F32, name="out_sb")
@@ -103,9 +105,6 @@ def tile_clusternet_pa_kernel(tc, xn, mu, out):
             for h in range(2):
                 copy_words_out(xt_grouped[:, g, 2 * h * P:(2 * h + 2) * P, :], banks[("xt", g, h)], 2 * P)
 
-        def quantise_features(g):
-            quantise(xt_codes[:, g, :], xt_scales[:, g, :], xt_grouped[:, g, :, :].rearrange("p c t -> p (c t)"))
-
         def regroup(copy, g, d0, d1):
             copy(out=x_grouped[:, g, d0:d1, :].rearrange("p (c i) j -> p c j i", i=4),
                  in_=x_sb[:, g, :, d0:d1].rearrange("p j (c i) -> p c j i", i=4))
@@ -119,6 +118,11 @@ def tile_clusternet_pa_kernel(tc, xn, mu, out):
         def quantise_rows(g, d0, d1):
             quantise(x_codes[:, g, d0:d1], x_scales[:, g, d0:d1],
                      x_grouped[:, g, d0:d1, :].rearrange("p d j -> p (d j)"))
+
+        def quantise_two_groups(codes, scales, grouped, g):
+            quantise(codes[:, g:g + 2, :].rearrange("p g c -> p (g c)"),
+                     scales[:, g:g + 2, :].rearrange("p g c -> p (g c)"),
+                     grouped[:, g:g + 2, :, :].rearrange("p g c t -> p (g c t)"))
 
         def first_matmul(g):
             logits = rotating.tile([P, PACK, K], F32, name="logits", tag="bank")
@@ -162,13 +166,13 @@ def tile_clusternet_pa_kernel(tc, xn, mu, out):
         def quantise_r(g):
             quantise(r_codes[:, g, :], r_scales[:, g, :], r_grouped[:, g, :, :].rearrange("p k j -> p (k j)"))
 
-        def second_matmul(g):
-            for half in range(2):
-                nc.tensor.matmul_mx(out=banks[("acc", half)][:],
+        def second_matmul(g, blocks=(0, 1, 2)):
+            for b in blocks:
+                d0, d1 = BLOCKS[b]
+                nc.tensor.matmul_mx(out=banks[("acc", b)][:],
                                     lhsT=r_codes[:, g, :].bitcast(FP8X4), lhsT_scale=r_scales[:, g, :],
-                                    rhs=x_codes[:, g, half * HALF:(half + 1) * HALF].bitcast(FP8X4),
-                                    rhs_scale=x_scales[:, g, half * HALF:(half + 1) * HALF],
-                                    start=(g == 0), stop=(g == G - 1))
+                                    rhs=x_codes[:, g, d0:d1].bitcast(FP8X4), rhs_scale=x_scales[:, g, d0:d1],
+                                    start=(g == 0), stop=(g == LAST_GROUP[b]))
 
         ctx.enter_context(tc.manual_schedule())
 
@@ -198,10 +202,12 @@ def tile_clusternet_pa_kernel(tc, xn, mu, out):
                 regroup(nc.vector.tensor_copy, g, QUARTER if g < SCALAR_HELPS else 0, D)
             if g == MU_STEP + 2:
                 quantise(mu_codes[:], mu_scales[:], mu_grouped[:].rearrange("p c t -> p (c t)"))
-            if 1 <= g <= STAGE1_GROUPS:
-                quantise_rows(g - 1, 0, D)
-            if g >= 1:
-                quantise_features(g - 1)
+            if g in (2, 4):
+                quantise_two_groups(x_codes, x_scales, x_grouped, g - 2)
+            if g >= 2 and g % 2 == 0:
+                quantise_two_groups(xt_codes, xt_scales, xt_grouped, g - 2)
+            if g == 6:
+                quantise_rows(4, 0, D)
 
         for g in range(G):
             first_matmul(g)
@@ -212,6 +218,7 @@ def tile_clusternet_pa_kernel(tc, xn, mu, out):
         for g in range(G):
             row_maximum(g)
         regroup(nc.scalar.copy, SCALAR_GROUP, 0, 3 * QUARTER)
+        regroup(nc.scalar.copy, *SCALAR_LAST_PIECE)
         bias(0, 1)
         regroup(nc.scalar.copy, SCALAR_GROUP, 3 * QUARTER, D)
         bias(1, 2)
@@ -220,15 +227,18 @@ def tile_clusternet_pa_kernel(tc, xn, mu, out):
             if g in BIASES_BEHIND:
                 bias(*BIASES_BEHIND[g])
 
-        for i in range(WARM_PASSES):
-            warm_bank = rotating.tile([P, D], F32, name="warm_bank", tag="bank")
-            nc.tensor.matmul_mx(out=warm_bank[:],
+        def warm_pass(bank):
+            nc.tensor.matmul_mx(out=bank[:],
                                 lhsT=x_codes[:, 0, 0:P].bitcast(FP8X4), lhsT_scale=x_scales[:, 0, 0:P],
                                 rhs=x_codes[:, 0, :].bitcast(FP8X4), rhs_scale=x_scales[:, 0, :],
                                 start=True, stop=True)
+
+        for i in range(WARM_PASSES):
+            warm_bank = rotating.tile([P, D], F32, name="warm_bank", tag="bank")
+            warm_pass(warm_bank)
         banks["colsum"] = rotating.tile([P, P], F32, name="r_transposed", tag="bank")
-        for half in range(2):
-            banks[("acc", half)] = rotating.tile([P, HALF], F32, name="acc", tag="bank")
+        for b, (d0, d1) in enumerate(BLOCKS):
+            banks[("acc", b)] = rotating.tile([P, d1 - d0], F32, name="acc", tag="bank")
 
         reciprocals(0, 2)
         quantise_rows(5, 0, D)
@@ -240,41 +250,53 @@ def tile_clusternet_pa_kernel(tc, xn, mu, out):
         normalise(2)
         normalise(3)
         reciprocals(4, 6)
-        quantise_r(0)
-        quantise_r(1)
-        cast_r(nc.vector.tensor_copy, 2)
+        quantise_two_groups(r_codes, r_scales, r_grouped, 0)
         normalise(4)
         normalise(5)
+        quantise_rows(6, 0, HALF)
         reciprocals(6, 8)
-        quantise_r(2)
-        quantise_rows(6, 0, D)
+        quantise_rows(6, HALF, D)
         normalise(6)
         normalise(7)
-        quantise_rows(7, 0, HALF)
-        regroup(nc.scalar.copy, *SCALAR_LAST_PIECE)
-        for g in range(VECTOR_CASTS, G):
+
+        for g in range(2, G - 1):
             cast_r(nc.scalar.copy, g)
-        for g in range(4):
-            add_to_colsum(g)
+
+        add_to_colsum(0)
+        add_to_colsum(1)
+        warm_pass(warm_bank)
+        warm_pass(warm_bank)
+        add_to_colsum(2)
+        add_to_colsum(3)
         second_matmul(0)
         second_matmul(1)
-        add_to_colsum(4)
-        add_to_colsum(5)
-        second_matmul(2)
-        add_to_colsum(6)
-        add_to_colsum(7)
-        quantise_r(3)
-        quantise_r(4)
-        quantise_rows(7, HALF, D)
-        quantise_r(5)
-        quantise_r(6)
-        nc.vector.tensor_reduce(out=col_sums[:], in_=banks["colsum"][:], axis=AX.X, op=ALU.add)
-        quantise_r(7)
-        nc.vector.reciprocal(col_recip[:], col_sums[:])
-        for g in range(3, G):
-            second_matmul(g)
+        for g in range(4, G):
+            add_to_colsum(g)
+        warm_pass(warm_bank)
 
-        nc.scalar.activation(out=out_sb[:, 0:HALF], in_=banks[("acc", 0)][:], func=AF.Copy, scale=col_recip[:, 0:1])
-        nc.sync.dma_start(out=out[:, 0:HALF], in_=out_sb[:, 0:HALF])
-        nc.vector.tensor_scalar_mul(out=out_sb[:, HALF:D], in0=banks[("acc", 1)][:], scalar1=col_recip[:, 0:1])
-        nc.sync.dma_start(out=out[:, HALF:D], in_=out_sb[:, HALF:D])
+        nc.scalar.activation(out=colsum_copy[:], in_=banks["colsum"][:], func=AF.Copy, accum_out=col_sums[:])
+
+        quantise_rows(7, 0, HALF)
+        cast_r(nc.vector.tensor_copy, 7)
+        quantise_rows(7, HALF, 3 * QUARTER)
+        quantise_two_groups(r_codes, r_scales, r_grouped, 2)
+        quantise_r(7)
+        for g in (4, 5, 6):
+            quantise_r(g)
+        quantise_rows(7, 3 * QUARTER, D)
+        nc.vector.reciprocal(col_recip[:], col_sums[:])
+
+        for g in (2, 3, 4):
+            second_matmul(g)
+        second_matmul(7, (0, 1))
+        second_matmul(5)
+        second_matmul(6)
+        second_matmul(7, (2,))
+
+        for b, (d0, d1) in enumerate(BLOCKS):
+            if b == 0:
+                nc.scalar.activation(out=out_sb[:, d0:d1], in_=banks[("acc", b)][:], func=AF.Copy,
+                                     scale=col_recip[:, 0:1])
+            else:
+                nc.vector.tensor_scalar_mul(out=out_sb[:, d0:d1], in0=banks[("acc", b)][:], scalar1=col_recip[:, 0:1])
+            nc.sync.dma_start(out=out[:, d0:d1], in_=out_sb[:, d0:d1])

@@ -35,7 +35,6 @@ LAST_GROUP = (6, 6, 7)
 
 BIASES_BEHIND = {0: (2, 3), 1: (3, 5), 3: (5, 8)}
 
-WARM_PASSES = 4
 MU_STEP = 2
 
 FLOPS = 2 * 2 * N_ROWS * D * K
@@ -157,7 +156,7 @@ def tile_clusternet_pa_kernel(tc, xn, mu, out):
 
         def add_to_colsum(g):
             for j in range(PACK):
-                nc.tensor.matmul(out=banks["colsum"][:], lhsT=r_f32[:, g, j, :], rhs=ident[:], is_transpose=True,
+                nc.tensor.matmul(out=banks["colsum"][:, 0:P], lhsT=r_f32[:, g, j, :], rhs=ident[:], is_transpose=True,
                                  start=(g == 0 and j == 0), stop=(g == G - 1 and j == PACK - 1))
 
         def cast_r(copy, g):
@@ -169,7 +168,7 @@ def tile_clusternet_pa_kernel(tc, xn, mu, out):
         def second_matmul(g, blocks=(0, 1, 2)):
             for b in blocks:
                 d0, d1 = BLOCKS[b]
-                nc.tensor.matmul_mx(out=banks[("acc", b)][:],
+                nc.tensor.matmul_mx(out=banks[("acc", b)][:, 0:d1 - d0],
                                     lhsT=r_codes[:, g, :].bitcast(FP8X4), lhsT_scale=r_scales[:, g, :],
                                     rhs=x_codes[:, g, d0:d1].bitcast(FP8X4), rhs_scale=x_scales[:, g, d0:d1],
                                     start=(g == 0), stop=(g == LAST_GROUP[b]))
@@ -222,7 +221,7 @@ def tile_clusternet_pa_kernel(tc, xn, mu, out):
         bias(0, 1)
         regroup(nc.scalar.copy, SCALAR_GROUP, 3 * QUARTER, D)
         bias(1, 2)
-        for g in range(G):
+        for g in range(G - 2):
             exponentials(g)
             if g in BIASES_BEHIND:
                 bias(*BIASES_BEHIND[g])
@@ -233,12 +232,10 @@ def tile_clusternet_pa_kernel(tc, xn, mu, out):
                                 rhs=x_codes[:, 0, :].bitcast(FP8X4), rhs_scale=x_scales[:, 0, :],
                                 start=True, stop=True)
 
-        for i in range(WARM_PASSES):
-            warm_bank = rotating.tile([P, D], F32, name="warm_bank", tag="bank")
-            warm_pass(warm_bank)
-        banks["colsum"] = rotating.tile([P, P], F32, name="r_transposed", tag="bank")
-        for b, (d0, d1) in enumerate(BLOCKS):
-            banks[("acc", b)] = rotating.tile([P, d1 - d0], F32, name="acc", tag="bank")
+        for what in ("colsum", ("acc", 0), ("acc", 1), ("acc", 2)):
+            banks[what] = rotating.tile([P, D], F32, name="sums", tag="bank")
+            warm_pass(banks[what])
+        spare = rotating.tile([P, D], F32, name="spare", tag="bank")
 
         reciprocals(0, 2)
         quantise_rows(5, 0, D)
@@ -249,54 +246,59 @@ def tile_clusternet_pa_kernel(tc, xn, mu, out):
         cast_r(nc.vector.tensor_copy, 1)
         normalise(2)
         normalise(3)
-        reciprocals(4, 6)
-        quantise_two_groups(r_codes, r_scales, r_grouped, 0)
-        normalise(4)
-        normalise(5)
-        quantise_rows(6, 0, HALF)
-        reciprocals(6, 8)
-        quantise_rows(6, HALF, D)
-        normalise(6)
-        normalise(7)
-
-        for g in range(2, G - 1):
-            cast_r(nc.scalar.copy, g)
-
+        cast_r(nc.scalar.copy, 2)
+        exponentials(6)
+        exponentials(7)
+        cast_r(nc.scalar.copy, 3)
         add_to_colsum(0)
         add_to_colsum(1)
-        warm_pass(warm_bank)
-        warm_pass(warm_bank)
+        warm_pass(spare)
+        warm_pass(spare)
         add_to_colsum(2)
         add_to_colsum(3)
+
+        reciprocals(4, 6)
+        quantise_two_groups(r_codes, r_scales, r_grouped, 0)
+        quantise_rows(6, 0, HALF)
+        normalise(4)
+        normalise(5)
         second_matmul(0)
         second_matmul(1)
-        for g in range(4, G):
-            add_to_colsum(g)
-        warm_pass(warm_bank)
+        add_to_colsum(4)
+        add_to_colsum(5)
+        warm_pass(spare)
 
-        nc.scalar.activation(out=colsum_copy[:], in_=banks["colsum"][:], func=AF.Copy, accum_out=col_sums[:])
-
+        quantise_r(2)
+        reciprocals(6, 7)
+        quantise_rows(6, HALF, D)
+        normalise(6)
+        reciprocals(7, 8)
         quantise_rows(7, 0, HALF)
-        cast_r(nc.vector.tensor_copy, 7)
-        quantise_rows(7, HALF, 3 * QUARTER)
-        quantise_two_groups(r_codes, r_scales, r_grouped, 2)
-        quantise_r(7)
+        normalise(7)
         for g in (4, 5, 6):
-            quantise_r(g)
-        quantise_rows(7, 3 * QUARTER, D)
-        nc.vector.reciprocal(col_recip[:], col_sums[:])
+            cast_r(nc.scalar.copy, g)
+        second_matmul(2)
+        add_to_colsum(6)
+        add_to_colsum(7)
+        nc.scalar.activation(out=colsum_copy[:], in_=banks["colsum"][:, 0:P], func=AF.Copy, accum_out=col_sums[:])
 
-        for g in (2, 3, 4):
+        quantise_r(3)
+        quantise_rows(7, HALF, 3 * QUARTER)
+        cast_r(nc.vector.tensor_copy, 7)
+        for g in (4, 5, 7, 6):
+            quantise_r(g)
+        nc.vector.reciprocal(col_recip[:], col_sums[:])
+        quantise_rows(7, 3 * QUARTER, D)
+        for g in (3, 4, 5):
             second_matmul(g)
         second_matmul(7, (0, 1))
-        second_matmul(5)
         second_matmul(6)
         second_matmul(7, (2,))
 
         for b, (d0, d1) in enumerate(BLOCKS):
             if b == 0:
-                nc.scalar.activation(out=out_sb[:, d0:d1], in_=banks[("acc", b)][:], func=AF.Copy,
+                nc.scalar.activation(out=out_sb[:, d0:d1], in_=banks[("acc", b)][:, 0:d1 - d0], func=AF.Copy,
                                      scale=col_recip[:, 0:1])
             else:
-                nc.vector.tensor_scalar_mul(out=out_sb[:, d0:d1], in0=banks[("acc", b)][:], scalar1=col_recip[:, 0:1])
+                nc.vector.tensor_scalar_mul(out=out_sb[:, d0:d1], in0=banks[("acc", b)][:, 0:d1 - d0], scalar1=col_recip[:, 0:1])
             nc.sync.dma_start(out=out[:, d0:d1], in_=out_sb[:, d0:d1])

@@ -24,14 +24,10 @@ BANKS = 8
 
 QUARTER = D // 4
 HALF = D // 2
-STAGE1_GROUPS = 5
 SCALAR_HELPS = 4
-SCALAR_GROUP = 5
 GPSIMD_PIECES = ((6, 0, HALF), (6, HALF, D), (7, 0, HALF))
-SCALAR_LAST_PIECE = (7, HALF, D)
 
-BLOCKS = ((0, HALF), (HALF, 3 * QUARTER), (3 * QUARTER, D))
-LAST_GROUP = (6, 6, 7)
+LAST_GROUP = 5
 
 BIASES_BEHIND = {0: (2, 3), 1: (3, 5), 3: (5, 8)}
 
@@ -70,7 +66,6 @@ def tile_clusternet_pa_kernel(tc, xn, mu, out):
         table_in = keep.tile([P, 1], F32, name="table_in")
         table_out = keep.tile([P, 1], F32, name="table_out")
         one_zero = keep.tile([P, 2], F32, name="one_zero")
-        colsum_copy = keep.tile([P, P], F32, name="colsum_copy")
         col_sums = keep.tile([P, 1], F32, name="col_sums")
         col_recip = keep.tile([P, 1], F32, name="col_recip")
         out_sb = keep.tile([P, D], F32, name="out_sb")
@@ -114,14 +109,12 @@ def tile_clusternet_pa_kernel(tc, xn, mu, out):
                                     scalar1=one_zero[:, 0:1], scalar2=one_zero[:, 1:2],
                                     op0=ALU.mult, op1=ALU.add)
 
+        def quantise_features(g):
+            quantise(xt_codes[:, g, :], xt_scales[:, g, :], xt_grouped[:, g, :, :].rearrange("p c t -> p (c t)"))
+
         def quantise_rows(g, d0, d1):
             quantise(x_codes[:, g, d0:d1], x_scales[:, g, d0:d1],
                      x_grouped[:, g, d0:d1, :].rearrange("p d j -> p (d j)"))
-
-        def quantise_two_groups(codes, scales, grouped, g):
-            quantise(codes[:, g:g + 2, :].rearrange("p g c -> p (g c)"),
-                     scales[:, g:g + 2, :].rearrange("p g c -> p (g c)"),
-                     grouped[:, g:g + 2, :, :].rearrange("p g c t -> p (g c t)"))
 
         def first_matmul(g):
             logits = rotating.tile([P, PACK, K], F32, name="logits", tag="bank")
@@ -165,13 +158,13 @@ def tile_clusternet_pa_kernel(tc, xn, mu, out):
         def quantise_r(g):
             quantise(r_codes[:, g, :], r_scales[:, g, :], r_grouped[:, g, :, :].rearrange("p k j -> p (k j)"))
 
-        def second_matmul(g, blocks=(0, 1, 2)):
-            for b in blocks:
-                d0, d1 = BLOCKS[b]
-                nc.tensor.matmul_mx(out=banks[("acc", b)][:, 0:d1 - d0],
+        def second_matmul(g):
+            for half in range(2):
+                d0, d1 = half * HALF, (half + 1) * HALF
+                nc.tensor.matmul_mx(out=banks[("acc", half)][:, 0:HALF],
                                     lhsT=r_codes[:, g, :].bitcast(FP8X4), lhsT_scale=r_scales[:, g, :],
                                     rhs=x_codes[:, g, d0:d1].bitcast(FP8X4), rhs_scale=x_scales[:, g, d0:d1],
-                                    start=(g == 0), stop=(g == LAST_GROUP[b]))
+                                    start=(g == 0), stop=(g == LAST_GROUP))
 
         ctx.enter_context(tc.manual_schedule())
 
@@ -197,16 +190,16 @@ def tile_clusternet_pa_kernel(tc, xn, mu, out):
                 copy_group_out(g - 1)
             if g == MU_STEP + 1:
                 copy_words_out(mu_grouped[:, :, :], mu_bank, P)
-            if g < STAGE1_GROUPS:
-                regroup(nc.vector.tensor_copy, g, QUARTER if g < SCALAR_HELPS else 0, D)
+            if g < SCALAR_HELPS:
+                regroup(nc.vector.tensor_copy, g, QUARTER, D)
+            if g == SCALAR_HELPS + 1:
+                regroup(nc.vector.tensor_copy, SCALAR_HELPS, 3 * QUARTER, D)
             if g == MU_STEP + 2:
                 quantise(mu_codes[:], mu_scales[:], mu_grouped[:].rearrange("p c t -> p (c t)"))
-            if g in (2, 4):
-                quantise_two_groups(x_codes, x_scales, x_grouped, g - 2)
-            if g >= 2 and g % 2 == 0:
-                quantise_two_groups(xt_codes, xt_scales, xt_grouped, g - 2)
-            if g == 6:
-                quantise_rows(4, 0, D)
+            if 1 <= g <= SCALAR_HELPS:
+                quantise_rows(g - 1, 0, D)
+            if g >= 1:
+                quantise_features(g - 1)
 
         for g in range(G):
             first_matmul(g)
@@ -216,12 +209,11 @@ def tile_clusternet_pa_kernel(tc, xn, mu, out):
             regroup_on_gpsimd(*piece)
         for g in range(G):
             row_maximum(g)
-        regroup(nc.scalar.copy, SCALAR_GROUP, 0, 3 * QUARTER)
-        regroup(nc.scalar.copy, *SCALAR_LAST_PIECE)
+        regroup(nc.scalar.copy, 4, 0, HALF)
         bias(0, 1)
-        regroup(nc.scalar.copy, SCALAR_GROUP, 3 * QUARTER, D)
+        regroup(nc.scalar.copy, 4, HALF, 3 * QUARTER)
         bias(1, 2)
-        for g in range(G - 2):
+        for g in range(G):
             exponentials(g)
             if g in BIASES_BEHIND:
                 bias(*BIASES_BEHIND[g])
@@ -232,13 +224,14 @@ def tile_clusternet_pa_kernel(tc, xn, mu, out):
                                 rhs=x_codes[:, 0, :].bitcast(FP8X4), rhs_scale=x_scales[:, 0, :],
                                 start=True, stop=True)
 
-        for what in ("colsum", ("acc", 0), ("acc", 1), ("acc", 2)):
+        for what in ("colsum", ("acc", 0), ("acc", 1)):
             banks[what] = rotating.tile([P, D], F32, name="sums", tag="bank")
             warm_pass(banks[what])
         spare = rotating.tile([P, D], F32, name="spare", tag="bank")
+        warm_pass(spare)
 
         reciprocals(0, 2)
-        quantise_rows(5, 0, D)
+        quantise_rows(6, 0, HALF)
         normalise(0)
         normalise(1)
         reciprocals(2, 4)
@@ -246,10 +239,6 @@ def tile_clusternet_pa_kernel(tc, xn, mu, out):
         cast_r(nc.vector.tensor_copy, 1)
         normalise(2)
         normalise(3)
-        cast_r(nc.scalar.copy, 2)
-        exponentials(6)
-        exponentials(7)
-        cast_r(nc.scalar.copy, 3)
         add_to_colsum(0)
         add_to_colsum(1)
         warm_pass(spare)
@@ -258,8 +247,9 @@ def tile_clusternet_pa_kernel(tc, xn, mu, out):
         add_to_colsum(3)
 
         reciprocals(4, 6)
-        quantise_two_groups(r_codes, r_scales, r_grouped, 0)
-        quantise_rows(6, 0, HALF)
+        quantise_r(0)
+        quantise_r(1)
+        cast_r(nc.vector.tensor_copy, 2)
         normalise(4)
         normalise(5)
         second_matmul(0)
@@ -268,37 +258,42 @@ def tile_clusternet_pa_kernel(tc, xn, mu, out):
         add_to_colsum(5)
         warm_pass(spare)
 
-        quantise_r(2)
-        reciprocals(6, 7)
         quantise_rows(6, HALF, D)
-        normalise(6)
-        reciprocals(7, 8)
+        reciprocals(6, 8)
+        quantise_r(2)
         quantise_rows(7, 0, HALF)
+        normalise(6)
         normalise(7)
-        for g in (4, 5, 6):
-            cast_r(nc.scalar.copy, g)
         second_matmul(2)
         add_to_colsum(6)
         add_to_colsum(7)
-        nc.scalar.activation(out=colsum_copy[:], in_=banks["colsum"][:, 0:P], func=AF.Copy, accum_out=col_sums[:])
 
+        cast_r(nc.scalar.copy, 3)
+        cast_r(nc.scalar.copy, 4)
+        regroup(nc.scalar.copy, 5, 0, D)
+        regroup(nc.scalar.copy, 7, HALF, D)
+        cast_r(nc.scalar.copy, 5)
+
+        quantise_rows(4, 0, D)
+        cast_r(nc.vector.tensor_copy, 6)
         quantise_r(3)
-        quantise_rows(7, HALF, 3 * QUARTER)
         cast_r(nc.vector.tensor_copy, 7)
-        for g in (4, 5, 7, 6):
-            quantise_r(g)
+        quantise_r(4)
+        second_matmul(3)
+        second_matmul(4)
+        nc.vector.tensor_reduce(out=col_sums[:], in_=banks["colsum"][:, 0:P], axis=AX.X, op=ALU.add)
+        quantise_r(6)
+        quantise_r(7)
         nc.vector.reciprocal(col_recip[:], col_sums[:])
-        quantise_rows(7, 3 * QUARTER, D)
-        for g in (3, 4, 5):
-            second_matmul(g)
-        second_matmul(7, (0, 1))
+        quantise_rows(5, 0, D)
+        quantise_rows(7, HALF, D)
+        quantise_r(5)
         second_matmul(6)
-        second_matmul(7, (2,))
+        second_matmul(7)
+        second_matmul(5)
 
-        for b, (d0, d1) in enumerate(BLOCKS):
-            if b == 0:
-                nc.scalar.activation(out=out_sb[:, d0:d1], in_=banks[("acc", b)][:, 0:d1 - d0], func=AF.Copy,
-                                     scale=col_recip[:, 0:1])
-            else:
-                nc.vector.tensor_scalar_mul(out=out_sb[:, d0:d1], in0=banks[("acc", b)][:, 0:d1 - d0], scalar1=col_recip[:, 0:1])
-            nc.sync.dma_start(out=out[:, d0:d1], in_=out_sb[:, d0:d1])
+        nc.scalar.activation(out=out_sb[:, 0:HALF], in_=banks[("acc", 0)][:, 0:HALF], func=AF.Copy,
+                             scale=col_recip[:, 0:1])
+        nc.sync.dma_start(out=out[:, 0:HALF], in_=out_sb[:, 0:HALF])
+        nc.vector.tensor_scalar_mul(out=out_sb[:, HALF:D], in0=banks[("acc", 1)][:, 0:HALF], scalar1=col_recip[:, 0:1])
+        nc.sync.dma_start(out=out[:, HALF:D], in_=out_sb[:, HALF:D])

from contextlib import ExitStack

import concourse.mybir as mybir
from concourse.masks import make_identity

F32 = mybir.dt.float32
BF16 = mybir.dt.bfloat16
U32 = mybir.dt.uint32
U8 = mybir.dt.uint8
FP8X4 = mybir.dt.float8_e4m3fn_x4
AF = mybir.ActivationFunctionType
ALU = mybir.AluOpType
AX = mybir.AxisListType

P = 128
PACK = 4
N_ROWS = 4096
D = 512
K = 128
BETA = 5.0
G = N_ROWS // (P * PACK)

BANKS = 8

QUARTER = D // 4
HALF = D // 2
SCALAR_HELPS = 4
GPSIMD_PIECES = ((6, 0, HALF), (6, HALF, D), (7, 0, HALF))

LAST_GROUP = 5

BIASES_BEHIND = {0: (2, 3), 1: (3, 5), 3: (5, 8)}

MU_STEP = 2

FLOPS = 2 * 2 * N_ROWS * D * K


def tile_clusternet_pa_kernel(tc, xn, mu, out):
    nc = tc.nc
    with ExitStack() as ctx:
        keep = ctx.enter_context(tc.tile_pool(name="keep", bufs=1))
        rotating = ctx.enter_context(tc.psum_pool(name="rotating", bufs=BANKS))

        x_sb = keep.tile([P, G, PACK, D], BF16, name="x_sb")
        mu_sb = keep.tile([P, D], BF16, name="mu_sb")
        ident = keep.tile([P, P], F32, name="ident")
        xt_grouped = keep.tile([P, G, PACK * P, PACK], BF16, name="xt_grouped", align_bytes=64)
        xt_codes = keep.tile([P, G, PACK * P], U32, name="xt_codes", align_bytes=64)
        xt_scales = keep.tile([P, G, PACK * P], U8, name="xt_scales", align_bytes=64)
        mu_grouped = keep.tile([P, K, PACK], BF16, name="mu_grouped", align_bytes=64)
        mu_codes = keep.tile([P, K], U32, name="mu_codes", align_bytes=64)
        mu_scales = keep.tile([P, K], U8, name="mu_scales", align_bytes=64)
        x_grouped = keep.tile([P, G, D, PACK], BF16, name="x_grouped", align_bytes=64)
        x_codes = keep.tile([P, G, D], U32, name="x_codes", align_bytes=64)
        x_scales = keep.tile([P, G, D], U8, name="x_scales", align_bytes=64)
        e_sb = keep.tile([P, G, PACK, K], F32, name="e_sb")
        r_f32 = keep.tile([P, G, PACK, K], F32, name="r_f32")
        r_grouped = keep.tile([P, G, K, PACK], BF16, name="r_grouped", align_bytes=64)
        r_codes = keep.tile([P, G, K], U32, name="r_codes", align_bytes=64)
        r_scales = keep.tile([P, G, K], U8, name="r_scales", align_bytes=64)
        row_maxima = keep.tile([P, G, PACK], F32, name="row_maxima")
        exp_bias = keep.tile([P, G, PACK], F32, name="exp_bias")
        row_sums = keep.tile([P, G, PACK], F32, name="row_sums")
        row_recip = keep.tile([P, G, PACK], F32, name="row_recip")
        table_in = keep.tile([P, 1], F32, name="table_in")
        table_out = keep.tile([P, 1], F32, name="table_out")
        one_zero = keep.tile([P, 2], F32, name="one_zero")
        col_sums = keep.tile([P, 1], F32, name="col_sums")
        col_recip = keep.tile([P, 1], F32, name="col_recip")
        out_sb = keep.tile([P, D], F32, name="out_sb")

        banks = {}

        def load_rows(g, j0, j1):
            rows = xn[g * P * PACK:(g + 1) * P * PACK, :].rearrange("(p j) d -> p j d", j=PACK)
            nc.sync.dma_start(out=x_sb[:, g, j0:j1, :], in_=rows[:, j0:j1, :])

        def transpose_words(bank, column, bf16_rows):
            words = bf16_rows.bitcast(F32)
            for u in range(2):
                nc.tensor.transpose(bank[:, u, column:column + P], words[:, u * P:(u + 1) * P], ident[:])

        def copy_words_out(grouped, bank, columns):
            dst = grouped.rearrange("p c t -> p (c t)").bitcast(F32).rearrange("p (c u) -> p c u", u=2)
            nc.scalar.copy(out=dst, in_=bank[:, :, 0:columns].rearrange("p u c -> p c u"))

        def quantise(codes, scales, grouped):
            nc.vector.quantize_mx(out=codes.bitcast(FP8X4), scales=scales, in_=grouped)

        def transpose_group(g):
            for h in range(2):
                bank = rotating.tile([P, 2, 2 * P], F32, name="bank", tag="bank")
                banks[("xt", g, h)] = bank
                for i in range(2):
                    transpose_words(bank, i * P, x_sb[:, g, 2 * h + i, :])

        def copy_group_out(g):
            for h in range(2):
                copy_words_out(xt_grouped[:, g, 2 * h * P:(2 * h + 2) * P, :], banks[("xt", g, h)], 2 * P)

        def regroup(copy, g, d0, d1):
            copy(out=x_grouped[:, g, d0:d1, :].rearrange("p (c i) j -> p c j i", i=4),
                 in_=x_sb[:, g, :, d0:d1].rearrange("p j (c i) -> p c j i", i=4))

        def regroup_on_gpsimd(g, d0, d1):
            nc.gpsimd.tensor_scalar(out=x_grouped[:, g, d0:d1, :],
                                    in0=x_sb[:, g, :, d0:d1].rearrange("p j d -> p d j"),
                                    scalar1=one_zero[:, 0:1], scalar2=one_zero[:, 1:2],
                                    op0=ALU.mult, op1=ALU.add)

        def quantise_features(g):
            quantise(xt_codes[:, g, :], xt_scales[:, g, :], xt_grouped[:, g, :, :].rearrange("p c t -> p (c t)"))

        def quantise_rows(g, d0, d1):
            quantise(x_codes[:, g, d0:d1], x_scales[:, g, d0:d1],
                     x_grouped[:, g, d0:d1, :].rearrange("p d j -> p (d j)"))

        def first_matmul(g):
            logits = rotating.tile([P, PACK, K], F32, name="logits", tag="bank")
            banks[("logits", g)] = logits
            for j in range(PACK):
                nc.tensor.matmul_mx(out=logits[:, j, :],
                                    lhsT=xt_codes[:, g, j * P:(j + 1) * P].bitcast(FP8X4),
                                    lhsT_scale=xt_scales[:, g, j * P:(j + 1) * P],
                                    rhs=mu_codes[:].bitcast(FP8X4), rhs_scale=mu_scales[:],
                                    start=True, stop=True)

        def row_maximum(g):
            nc.vector.tensor_reduce(out=row_maxima[:, g, :], in_=banks[("logits", g)][:], axis=AX.X, op=ALU.max)

        def bias(g0, g1):
            nc.scalar.mul(exp_bias[:, g0:g1, :], row_maxima[:, g0:g1, :], -BETA)

        def exponentials(g):
            logits = banks[("logits", g)]
            for j in range(PACK):
                nc.scalar.activation(out=e_sb[:, g, j, :], in_=logits[:, j, :], func=AF.Exp,
                                     bias=exp_bias[:, g, j:j + 1], scale=BETA,
                                     accum_out=row_sums[:, g, j:j + 1])

        def reciprocals(g0, g1):
            nc.vector.reciprocal(row_recip[:, g0:g1, :], row_sums[:, g0:g1, :])

        def normalise(g):
            for j in range(PACK):
                nc.vector.tensor_scalar_mul(out=r_f32[:, g, j, :], in0=e_sb[:, g, j, :],
                                            scalar1=row_recip[:, g, j:j + 1])

        def add_to_colsum(g):
            for j in range(PACK):
                nc.tensor.matmul(out=banks["colsum"][:, 0:P], lhsT=r_f32[:, g, j, :], rhs=ident[:], is_transpose=True,
                                 start=(g == 0 and j == 0), stop=(g == G - 1 and j == PACK - 1))

        def cast_r(copy, g):
            copy(out=r_grouped[:, g, :, :], in_=r_f32[:, g, :, :].rearrange("p j k -> p k j"))

        def quantise_r(g):
            quantise(r_codes[:, g, :], r_scales[:, g, :], r_grouped[:, g, :, :].rearrange("p k j -> p (k j)"))

        def second_matmul(g):
            for half in range(2):
                d0, d1 = half * HALF, (half + 1) * HALF
                nc.tensor.matmul_mx(out=banks[("acc", half)][:, 0:HALF],
                                    lhsT=r_codes[:, g, :].bitcast(FP8X4), lhsT_scale=r_scales[:, g, :],
                                    rhs=x_codes[:, g, d0:d1].bitcast(FP8X4), rhs_scale=x_scales[:, g, d0:d1],
                                    start=(g == 0), stop=(g == LAST_GROUP))

        ctx.enter_context(tc.manual_schedule())

        load_rows(0, 0, PACK // 2)
        load_rows(0, PACK // 2, PACK)
        for g in range(1, G):
            load_rows(g, 0, PACK)
            if g == MU_STEP:
                nc.sync.dma_start(out=mu_sb[:], in_=mu[:, :])
        make_identity(nc, ident[:])
        nc.vector.memset(table_in[:], 0.0)
        nc.scalar.activation(out=table_out[:], in_=table_in[:], func=AF.Exp)

        for g in range(G + 1):
            if g < G:
                transpose_group(g)
            if g == MU_STEP:
                mu_bank = rotating.tile([P, 2, 2 * P], F32, name="bank", tag="bank")
                transpose_words(mu_bank, 0, mu_sb[:])
            if 1 <= g <= SCALAR_HELPS:
                regroup(nc.scalar.copy, g - 1, 0, QUARTER)
            if g >= 1:
                copy_group_out(g - 1)
            if g == MU_STEP + 1:
                copy_words_out(mu_grouped[:, :, :], mu_bank, P)
            if g < SCALAR_HELPS:
                regroup(nc.vector.tensor_copy, g, QUARTER, D)
            if g == SCALAR_HELPS + 1:
                regroup(nc.vector.tensor_copy, SCALAR_HELPS, 3 * QUARTER, D)
            if g == MU_STEP + 2:
                quantise(mu_codes[:], mu_scales[:], mu_grouped[:].rearrange("p c t -> p (c t)"))
            if 1 <= g <= SCALAR_HELPS:
                quantise_rows(g - 1, 0, D)
            if g >= 1:
                quantise_features(g - 1)

        for g in range(G):
            first_matmul(g)
        nc.vector.memset(one_zero[:, 0:1], 1.0)
        nc.vector.memset(one_zero[:, 1:2], 0.0)
        for piece in GPSIMD_PIECES:
            regroup_on_gpsimd(*piece)
        for g in range(G):
            row_maximum(g)
        regroup(nc.scalar.copy, 4, 0, HALF)
        bias(0, 1)
        regroup(nc.scalar.copy, 4, HALF, 3 * QUARTER)
        bias(1, 2)
        for g in range(G):
            exponentials(g)
            if g in BIASES_BEHIND:
                bias(*BIASES_BEHIND[g])

        def warm_pass(bank):
            nc.tensor.matmul_mx(out=bank[:],
                                lhsT=x_codes[:, 0, 0:P].bitcast(FP8X4), lhsT_scale=x_scales[:, 0, 0:P],
                                rhs=x_codes[:, 0, :].bitcast(FP8X4), rhs_scale=x_scales[:, 0, :],
                                start=True, stop=True)

        for what in ("colsum", ("acc", 0), ("acc", 1)):
            banks[what] = rotating.tile([P, D], F32, name="sums", tag="bank")
            warm_pass(banks[what])
        spare = rotating.tile([P, D], F32, name="spare", tag="bank")
        warm_pass(spare)

        reciprocals(0, 2)
        quantise_rows(6, 0, HALF)
        normalise(0)
        normalise(1)
        reciprocals(2, 4)
        cast_r(nc.vector.tensor_copy, 0)
        cast_r(nc.vector.tensor_copy, 1)
        normalise(2)
        normalise(3)
        add_to_colsum(0)
        add_to_colsum(1)
        warm_pass(spare)
        warm_pass(spare)
        add_to_colsum(2)
        add_to_colsum(3)

        reciprocals(4, 6)
        quantise_r(0)
        quantise_r(1)
        cast_r(nc.vector.tensor_copy, 2)
        normalise(4)
        normalise(5)
        second_matmul(0)
        second_matmul(1)
        add_to_colsum(4)
        add_to_colsum(5)
        warm_pass(spare)

        quantise_rows(6, HALF, D)
        reciprocals(6, 8)
        quantise_r(2)
        quantise_rows(7, 0, HALF)
        normalise(6)
        normalise(7)
        second_matmul(2)
        add_to_colsum(6)
        add_to_colsum(7)

        cast_r(nc.scalar.copy, 3)
        cast_r(nc.scalar.copy, 4)
        regroup(nc.scalar.copy, 5, 0, D)
        regroup(nc.scalar.copy, 7, HALF, D)
        cast_r(nc.scalar.copy, 5)

        quantise_rows(4, 0, D)
        cast_r(nc.vector.tensor_copy, 6)
        quantise_r(3)
        cast_r(nc.vector.tensor_copy, 7)
        quantise_r(4)
        second_matmul(3)
        second_matmul(4)
        nc.vector.tensor_reduce(out=col_sums[:], in_=banks["colsum"][:, 0:P], axis=AX.X, op=ALU.add)
        quantise_r(6)
        quantise_r(7)
        nc.vector.reciprocal(col_recip[:], col_sums[:])
        quantise_rows(5, 0, D)
        quantise_rows(7, HALF, D)
        quantise_r(5)
        second_matmul(6)
        second_matmul(7)
        second_matmul(5)

        nc.scalar.activation(out=out_sb[:, 0:HALF], in_=banks[("acc", 0)][:, 0:HALF], func=AF.Copy,
                             scale=col_recip[:, 0:1])
        nc.sync.dma_start(out=out[:, 0:HALF], in_=out_sb[:, 0:HALF])
        nc.vector.tensor_scalar_mul(out=out_sb[:, HALF:D], in0=banks[("acc", 1)][:, 0:HALF], scalar1=col_recip[:, 0:1])
        nc.sync.dma_start(out=out[:, HALF:D], in_=out_sb[:, HALF:D])
